import numpy as np
import ml_dtypes


def mxq(x, axis, fmt="e4m3"):
    dtype, down = {"e4m3": (ml_dtypes.float8_e4m3fn, 7), "e5m2": (ml_dtypes.float8_e5m2, 14)}[fmt]
    v = np.moveaxis(np.asarray(x, np.float32).astype(ml_dtypes.bfloat16).astype(np.float64), axis, -1)
    blocks = v.reshape(v.shape[:-1] + (-1, 32))
    amax = np.abs(blocks).max(-1, keepdims=True)
    byte = np.maximum(np.where(amax > 0, np.frexp(amax)[1] - 1 + 127, 0) - down, 1)
    scale = np.exp2(byte - 127.0)
    codes = (blocks / scale).astype(np.float32).astype(dtype).astype(np.float64)
    return np.moveaxis((codes * scale).reshape(v.shape), -1, axis)


WIDE = False


def mx_kscale(k):
    if not WIDE:
        return np.ones(k)
    levels = np.array([10, -10, 5, -5, 0])
    a = np.random.permutation(np.resize(levels, k // 512 * 4)).reshape(k // 512, 4)
    idx = np.arange(k)
    return np.exp2(a[idx // 512, idx % 128 // 32])


BF16 = ml_dtypes.bfloat16


def bf(x):
    return np.asarray(x, np.float32).astype(BF16)


def f64(x):
    return np.asarray(x).astype(np.float64)


B, C, H, W, KS, CO = 2, 32, 163, 163, 4, 128
OH, OW = H - KS + 1, W - KS + 1
Q = C * KS * KS


def unfold_patches(x, k):
    oh, ow = x.shape[2] - k + 1, x.shape[3] - k + 1
    rows = []
    for di in range(k):
        cols = [x[:, :, di:di + oh, dj:dj + ow] for dj in range(k)]
        rows.append(np.stack(cols, axis=-1))
    return np.stack(rows, axis=-2)


def wide_factors():
    s = mx_kscale(Q)
    hi, lo = np.log2(s.max()), np.log2(s.min())
    n = np.arange(C)
    phi = np.exp2(np.round(hi + (lo - hi) * np.minimum(n, C - n) / (C / 2)))
    c, h, w = np.ogrid[:C, :H, :W]
    m, di, dj = np.ogrid[:C, :KS, :KS]
    return phi[(c * OH * OW + h * OW + w) % C], phi[(m + di * OW + dj) % C].reshape(Q)


def setup_inputs():
    fx, fw = wide_factors()
    return {"x": bf(np.random.standard_normal((B, C, H, W)) * fx),
            "weights": bf(np.random.standard_normal((Q, CO)) / np.sqrt(Q) / fw[:, None]),
            "bias": bf(np.random.standard_normal(CO) * 0.3)}


def reference(x, weights, bias):
    patches = unfold_patches(f64(x), KS)
    patches = patches.reshape(B, OH, OW, Q)
    out = (mxq(patches, 3, "e4m3") @ mxq(f64(weights), 0, "e4m3")) + f64(bias)
    return np.transpose(out, (0, 3, 1, 2))

@@ -1,0 +1,221 @@
+from contextlib import ExitStack
+
+import concourse.mybir as mybir
+from concourse.masks import make_identity
+
+BF16 = mybir.dt.bfloat16
+F32 = mybir.dt.float32
+U32 = mybir.dt.uint32
+U8 = mybir.dt.uint8
+FP8X4 = mybir.dt.float8_e4m3fn_x4
+ACT = mybir.ActivationFunctionType
+
+FLOPS = 2 * 51200 * 512 * 128
+
+P = 128
+HW = 163
+ROWS = 64 * HW
+NT = 82
+CH = 8
+CL = CH * HW
+CLP = 1312
+CW = CL // 2
+NQ = CH * 40
+HI0 = 35
+PIECES = ((0, 12), (12, 24), (24, 32), (32, 44), (44, 52), (52, 64), (64, 72), (72, 81), (81, 82))
+S_SHARE = ((0, 1, 2), (0, 1, 2), (0, 1, 2), (0, 1, 2), (0, 1))
+
+
+def tile_conv2d_kernel(tc, x, weights, bias, out):
+    nc = tc.nc
+    x_rows = x.rearrange("b c h w -> (b c h) w")
+    of = out.rearrange("b o u v -> b o (u v)")
+
+    with ExitStack() as ctx:
+        const = ctx.enter_context(tc.tile_pool(name="const", bufs=1))
+        reppool = ctx.enter_context(tc.tile_pool(name="rep", bufs=3))
+        tpool = ctx.enter_context(tc.tile_pool(name="tp", bufs=4))
+        cpool = ctx.enter_context(tc.tile_pool(name="cp", bufs=4))
+        opool = ctx.enter_context(tc.tile_pool(name="op", bufs=2))
+        psum_t = ctx.enter_context(tc.psum_pool(name="pst", bufs=2))
+        psum_m = ctx.enter_context(tc.psum_pool(name="psm", bufs=6))
+
+        ident = const.tile([P, P], BF16)
+        make_identity(nc, ident[:])
+        zb = const.tile([P, P], BF16)
+        nc.vector.memset(zb[:], 0.0)
+        nc.scalar.dma_start(out=zb[0:1, :], in_=bias.rearrange("(o c) -> o c", o=1))
+        raw_w = const.tile([P, 4, P], BF16)
+        w_view = weights.rearrange("(m i j) o -> j m i o", i=4, j=4)
+        for dj in range(4):
+            nc.scalar.dma_start(out=raw_w[dj:P:4, :, :], in_=w_view[dj])
+
+        x_of_tile = {}
+        for i, (t0, t1) in enumerate(PIECES):
+            xp = const.tile([P, t1 - t0, HW], BF16, name="xp%d" % i)
+            r0 = min(P * t0, ROWS - P)
+            nc.sync.dma_start(
+                out=xp[:],
+                in_=x_rows[r0:r0 + P * (t1 - t0), :].rearrange("(t p) w -> p t w", p=P),
+            )
+            for t in range(t0, t1):
+                x_of_tile[t] = (xp, t - t0)
+
+        xt_lo = const.tile([P, ROWS], BF16)
+        xt_hi = const.tile([P, ROWS], BF16)
+        xt = [xt_lo, xt_hi]
+        w0s = [0, HI0]
+
+        def evac(gi, dst, src):
+            if gi == 0:
+                nc.vector.tensor_copy(out=dst, in_=src)
+            else:
+                nc.scalar.copy(out=dst, in_=src)
+
+        def transposes(tg0):
+            for gi in range(2):
+                pt = psum_t.tile([P, 4, P], BF16, name="pt")
+                n = min(4, NT - tg0)
+                for u in range(n):
+                    xp, tl = x_of_tile[tg0 + u]
+                    nc.tensor.transpose(pt[:, u, :], xp[:, tl, w0s[gi]:w0s[gi] + P], ident[:])
+                if n == 4:
+                    evac(gi, xt[gi][:, P * tg0:P * tg0 + 4 * P],
+                         pt[:].rearrange("p u r -> p (u r)"))
+                else:
+                    evac(gi, xt[gi][:, P * tg0:P * tg0 + P], pt[:, 0, :])
+                    evac(gi, xt[gi][:, P * tg0 + P:ROWS], pt[:, 1, 64:P])
+
+        def slot(k, gi):
+            if k >= 4:
+                return 19200 + ((k - 4) * 2 + gi) * CW
+            return 12800 + (k * 2 + gi) * CW
+
+        state = {"t": 0}
+        xrs = {}
+        ots = {}
+        tgs = {}
+
+        def stage_in(k):
+            need = (CL * (k + 1) - 1) // P
+            while state["t"] <= need:
+                transposes(state["t"])
+                state["t"] += 4
+            for gi in range(2):
+                col = slot(k, gi)
+                nc.sync.dma_start(
+                    out=of[1, :, col:col + CW],
+                    in_=xt[gi][:, CL * k:CL * (k + 1)].bitcast(F32),
+                )
+            xr = reppool.tile([P, 5, CLP], BF16, name="xr")
+            xr32 = xr[:].bitcast(F32)
+            for dj in range(4):
+                col = slot(k, 0)
+                nc.sync.dma_start(
+                    out=xr32[dj:P:4, 0:3, 0:CW],
+                    in_=of[1, dj:dj + 96, col:col + CW].rearrange("(j m) c -> m j c", m=32),
+                )
+                col = slot(k, 1)
+                r0 = 96 - HI0 + dj
+                nc.sync.dma_start(
+                    out=xr32[dj:P:4, 3:5, 0:CW],
+                    in_=of[1, r0:r0 + 64, col:col + CW].rearrange("(j m) c -> m j c", m=32),
+                )
+            xrs[k] = xr
+
+        def copies(k, g):
+            xr = xrs[k]
+            xr5 = xr[:, :, 0:CL].rearrange("p j (c e h) -> p j c e h", e=2, h=HW)
+            xw = xr[:].bitcast(F32)[:, :, 0:CW].rearrange("p j (c w) -> p j c w", w=HW)
+            tg = tpool.tile([P, 4, 4 * NQ], BF16, align_bytes=64, name="tg")
+            tg5 = tg[:].rearrange("p v (c e h) -> p v c e h", e=2, h=160)
+            tw = tg[:].bitcast(F32).rearrange("p v (c e w) -> p v c e w", e=2, w=80)
+            tg4 = tg[:].rearrange("p v (c h) -> p v c h", h=160)
+            xr4 = xr[:, :, 0:CL].rearrange("p j (c h) -> p j c h", h=HW)
+            a = 0
+            while a < 4:
+                phi, jb0 = divmod(4 * g + a, 5)
+                shared = a in S_SHARE[g]
+                n = 1
+                while (a + n < 4 and jb0 + n < 5 and ((a + n) in S_SHARE[g]) == shared):
+                    n += 1
+                if shared:
+                    par = phi % 2
+                    s0 = (par * HW + phi) // 2
+                    nc.scalar.copy(
+                        out=tw[:, a:a + n, :, par, :],
+                        in_=xw[:, jb0:jb0 + n, :, s0:s0 + 80],
+                    )
+                    nc.vector.tensor_copy(
+                        out=tg5[:, a:a + n, :, 1 - par, :],
+                        in_=xr5[:, jb0:jb0 + n, :, 1 - par, phi:phi + 160],
+                    )
+                else:
+                    nc.vector.tensor_copy(
+                        out=tg4[:, a:a + n, :, :],
+                        in_=xr4[:, jb0:jb0 + n, :, phi:phi + 160],
+                    )
+                a += n
+            tgs[(k, g)] = tg
+
+        def compute(k, g):
+            b = k // 4
+            base = (k % 4) * CH * 800
+            if g == 0:
+                ot_new = opool.tile([P, NQ, 20], F32, name="ot")
+                ots[k] = ot_new
+            ot = ots[k]
+            tg = tgs[(k, g)]
+            codes = cpool.tile([P, 4 * NQ], U32, align_bytes=64, name="codes")
+            scales = cpool.tile([P, 4 * NQ], U8, align_bytes=64, name="scales")
+            tflat = tg[:].rearrange("p v e -> p (v e)")
+            for (e0, e1) in ((0, 4096), (4096, 5120)):
+                nc.vector.quantize_mx(
+                    out=codes[:, e0 // 4:e1 // 4].bitcast(FP8X4),
+                    scales=scales[:, e0 // 4:e1 // 4],
+                    in_=tflat[:, e0:e1],
+                )
+            for (start, q0, lo) in ((0, 0, 0), (128, 128, 0), (192, 256, 64)):
+                acc = psum_m.tile([P, 4, P], F32, name="acc")
+                for v in range(4):
+                    s = v * NQ + start
+                    nc.tensor.matmul_mx(
+                        out=acc[:, v, :],
+                        lhsT=wcodes[:].bitcast(FP8X4), lhsT_scale=wscales[:],
+                        rhs=codes[:, s:s + P].bitcast(FP8X4), rhs_scale=scales[:, s:s + P],
+                        start=True, stop=True,
+                    )
+                n = P - lo
+                nc.scalar.activation(
+                    out=ot[:, q0:q0 + n, 4 * g:4 * g + 4],
+                    in_=acc[:, :, lo:P].rearrange("p v q -> p q v"),
+                    func=ACT.Identity, bias=bias_sb[:, 0:1], scale=1.0,
+                )
+                if g == 4:
+                    nc.scalar.dma_start(
+                        out=of[b, :, base + q0 * 20:base + (q0 + n) * 20],
+                        in_=ot[:, q0:q0 + n, :].rearrange("p q v -> p (q v)"),
+                    )
+
+        units = [(k, g) for k in range(8) for g in range(5)]
+        stage_in(0)
+        wg = const.tile([P, P, 4], BF16, align_bytes=64)
+        nc.vector.tensor_copy(out=wg[:], in_=raw_w[:].rearrange("p i o -> p o i"))
+        wcodes = const.tile([P, P], U32, align_bytes=64)
+        wscales = const.tile([P, P], U8, align_bytes=64)
+        nc.vector.quantize_mx(
+            out=wcodes[:].bitcast(FP8X4), scales=wscales[:],
+            in_=wg[:].rearrange("p o i -> p (o i)"),
+        )
+        pb = psum_t.tile([P, 4, P], BF16, name="pt")
+        nc.tensor.transpose(pb[:, 0, :], zb[:], ident[:])
+        bias_sb = const.tile([P, 1], F32)
+        nc.vector.tensor_copy(out=bias_sb[:], in_=pb[:, 0, 0:1])
+        stage_in(1)
+        copies(0, 0)
+        for i, (k, g) in enumerate(units):
+            if g == 0 and k + 2 < 8:
+                stage_in(k + 2)
+            if i + 1 < len(units):
+                copies(units[i + 1][0], units[i + 1][1])
+            compute(k, g)

@@ -16,7 +16,9 @@ P = 128
 HW = 163
 ROWS = 64 * HW
 NT = 82
+NG = 21
 CH = 8
+NK = 8
 CL = CH * HW
 CLP = 1312
 CW = CL // 2
@@ -24,6 +26,9 @@ NQ = CH * 40
 HI0 = 35
 PIECES = ((0, 12), (12, 24), (24, 32), (32, 44), (44, 52), (52, 64), (64, 72), (72, 81), (81, 82))
 S_SHARE = ((0, 1, 2), (0, 1, 2), (0, 1, 2), (0, 1, 2), (0, 1))
+LOOK = 2
+XR_BUFS = 2
+WINDOWS = ((0, 0, 0), (128, 128, 0), (192, 256, 64))
 
 
 def tile_conv2d_kernel(tc, x, weights, bias, out):
@@ -33,12 +38,13 @@ def tile_conv2d_kernel(tc, x, weights, bias, out):
 
     with ExitStack() as ctx:
         const = ctx.enter_context(tc.tile_pool(name="const", bufs=1))
-        reppool = ctx.enter_context(tc.tile_pool(name="rep", bufs=3))
-        tpool = ctx.enter_context(tc.tile_pool(name="tp", bufs=4))
-        cpool = ctx.enter_context(tc.tile_pool(name="cp", bufs=4))
+        reppool = ctx.enter_context(tc.tile_pool(name="rep", bufs=XR_BUFS))
+        tpool = ctx.enter_context(tc.tile_pool(name="tp", bufs=5))
+        cpool = ctx.enter_context(tc.tile_pool(name="cp", bufs=5))
         opool = ctx.enter_context(tc.tile_pool(name="op", bufs=2))
         psum_t = ctx.enter_context(tc.psum_pool(name="pst", bufs=2))
         psum_m = ctx.enter_context(tc.psum_pool(name="psm", bufs=6))
+        ctx.enter_context(tc.manual_schedule())
 
         ident = const.tile([P, P], BF16)
         make_identity(nc, ident[:])
@@ -51,7 +57,9 @@ def tile_conv2d_kernel(tc, x, weights, bias, out):
             nc.scalar.dma_start(out=raw_w[dj:P:4, :, :], in_=w_view[dj])
 
         x_of_tile = {}
-        for i, (t0, t1) in enumerate(PIECES):
+
+        def load_x(i):
+            t0, t1 = PIECES[i]
             xp = const.tile([P, t1 - t0, HW], BF16, name="xp%d" % i)
             r0 = min(P * t0, ROWS - P)
             nc.sync.dma_start(
@@ -72,13 +80,30 @@ def tile_conv2d_kernel(tc, x, weights, bias, out):
             else:
                 nc.scalar.copy(out=dst, in_=src)
 
-        def transposes(tg0):
+        pending = {}
+
+        def transposes_pe(j):
+            tg0 = 4 * j
+            n = min(4, NT - tg0)
+            pts = []
             for gi in range(2):
                 pt = psum_t.tile([P, 4, P], BF16, name="pt")
-                n = min(4, NT - tg0)
                 for u in range(n):
                     xp, tl = x_of_tile[tg0 + u]
                     nc.tensor.transpose(pt[:, u, :], xp[:, tl, w0s[gi]:w0s[gi] + P], ident[:])
+                pts.append(pt)
+            pending[j] = pts
+
+        def transposes(j):
+            transposes_pe(j)
+            transposes_out(j)
+
+        def transposes_out(j):
+            tg0 = 4 * j
+            n = min(4, NT - tg0)
+            pts = pending[j]
+            for gi in range(2):
+                pt = pts[gi]
                 if n == 4:
                     evac(gi, xt[gi][:, P * tg0:P * tg0 + 4 * P],
                          pt[:].rearrange("p u r -> p (u r)"))
@@ -91,22 +116,20 @@ def tile_conv2d_kernel(tc, x, weights, bias, out):
                 return 19200 + ((k - 4) * 2 + gi) * CW
             return 12800 + (k * 2 + gi) * CW
 
-        state = {"t": 0}
-        xrs = {}
-        ots = {}
-        tgs = {}
-
-        def stage_in(k):
-            need = (CL * (k + 1) - 1) // P
-            while state["t"] <= need:
-                transposes(state["t"])
-                state["t"] += 4
+        def park(k):
             for gi in range(2):
                 col = slot(k, gi)
                 nc.sync.dma_start(
                     out=of[1, :, col:col + CW],
                     in_=xt[gi][:, CL * k:CL * (k + 1)].bitcast(F32),
                 )
+
+        xrs = {}
+        ots = {}
+        tgs = {}
+        cds = {}
+
+        def reload(k):
             xr = reppool.tile([P, 5, CLP], BF16, name="xr")
             xr32 = xr[:].bitcast(F32)
             for dj in range(4):
@@ -127,11 +150,12 @@ def tile_conv2d_kernel(tc, x, weights, bias, out):
             xr = xrs[k]
             xr5 = xr[:, :, 0:CL].rearrange("p j (c e h) -> p j c e h", e=2, h=HW)
             xw = xr[:].bitcast(F32)[:, :, 0:CW].rearrange("p j (c w) -> p j c w", w=HW)
+            xr4 = xr[:, :, 0:CL].rearrange("p j (c h) -> p j c h", h=HW)
             tg = tpool.tile([P, 4, 4 * NQ], BF16, align_bytes=64, name="tg")
             tg5 = tg[:].rearrange("p v (c e h) -> p v c e h", e=2, h=160)
             tw = tg[:].bitcast(F32).rearrange("p v (c e w) -> p v c e w", e=2, w=80)
             tg4 = tg[:].rearrange("p v (c h) -> p v c h", h=160)
-            xr4 = xr[:, :, 0:CL].rearrange("p j (c h) -> p j c h", h=HW)
+            runs = []
             a = 0
             while a < 4:
                 phi, jb0 = divmod(4 * g + a, 5)
@@ -139,13 +163,11 @@ def tile_conv2d_kernel(tc, x, weights, bias, out):
                 n = 1
                 while (a + n < 4 and jb0 + n < 5 and ((a + n) in S_SHARE[g]) == shared):
                     n += 1
+                runs.append((a, n, phi, jb0, shared))
+                a += n
+            for (a, n, phi, jb0, shared) in runs:
                 if shared:
                     par = phi % 2
-                    s0 = (par * HW + phi) // 2
-                    nc.scalar.copy(
-                        out=tw[:, a:a + n, :, par, :],
-                        in_=xw[:, jb0:jb0 + n, :, s0:s0 + 80],
-                    )
                     nc.vector.tensor_copy(
                         out=tg5[:, a:a + n, :, 1 - par, :],
                         in_=xr5[:, jb0:jb0 + n, :, 1 - par, phi:phi + 160],
@@ -155,50 +177,76 @@ def tile_conv2d_kernel(tc, x, weights, bias, out):
                         out=tg4[:, a:a + n, :, :],
                         in_=xr4[:, jb0:jb0 + n, :, phi:phi + 160],
                     )
-                a += n
+            for (a, n, phi, jb0, shared) in runs:
+                if shared:
+                    par = phi % 2
+                    s0 = (par * HW + phi) // 2
+                    nc.scalar.copy(
+                        out=tw[:, a:a + n, :, par, :],
+                        in_=xw[:, jb0:jb0 + n, :, s0:s0 + 80],
+                    )
             tgs[(k, g)] = tg
 
-        def compute(k, g):
-            b = k // 4
-            base = (k % 4) * CH * 800
-            if g == 0:
-                ot_new = opool.tile([P, NQ, 20], F32, name="ot")
-                ots[k] = ot_new
-            ot = ots[k]
-            tg = tgs[(k, g)]
+        def new_codes(k, g):
             codes = cpool.tile([P, 4 * NQ], U32, align_bytes=64, name="codes")
             scales = cpool.tile([P, 4 * NQ], U8, align_bytes=64, name="scales")
-            tflat = tg[:].rearrange("p v e -> p (v e)")
-            for (e0, e1) in ((0, 4096), (4096, 5120)):
-                nc.vector.quantize_mx(
-                    out=codes[:, e0 // 4:e1 // 4].bitcast(FP8X4),
-                    scales=scales[:, e0 // 4:e1 // 4],
-                    in_=tflat[:, e0:e1],
-                )
-            for (start, q0, lo) in ((0, 0, 0), (128, 128, 0), (192, 256, 64)):
-                acc = psum_m.tile([P, 4, P], F32, name="acc")
-                for v in range(4):
-                    s = v * NQ + start
-                    nc.tensor.matmul_mx(
-                        out=acc[:, v, :],
-                        lhsT=wcodes[:].bitcast(FP8X4), lhsT_scale=wscales[:],
-                        rhs=codes[:, s:s + P].bitcast(FP8X4), rhs_scale=scales[:, s:s + P],
-                        start=True, stop=True,
-                    )
-                n = P - lo
-                nc.scalar.activation(
-                    out=ot[:, q0:q0 + n, 4 * g:4 * g + 4],
-                    in_=acc[:, :, lo:P].rearrange("p v q -> p q v"),
-                    func=ACT.Identity, bias=bias_sb[:, 0:1], scale=1.0,
-                )
-                if g == 4:
-                    nc.scalar.dma_start(
-                        out=of[b, :, base + q0 * 20:base + (q0 + n) * 20],
-                        in_=ot[:, q0:q0 + n, :].rearrange("p q v -> p (q v)"),
-                    )
+            cds[(k, g)] = (codes, scales)
 
-        units = [(k, g) for k in range(8) for g in range(5)]
-        stage_in(0)
+        def quantise(k, g, w0, w1):
+            codes, scales = cds[(k, g)]
+            tflat = tgs[(k, g)][:].rearrange("p v e -> p (v e)")
+            nc.vector.quantize_mx(
+                out=codes[:, w0:w1].bitcast(FP8X4), scales=scales[:, w0:w1],
+                in_=tflat[:, 4 * w0:4 * w1],
+            )
+
+        def passes(k, g, wi):
+            start, q0, lo = WINDOWS[wi]
+            codes, scales = cds[(k, g)]
+            acc = psum_m.tile([P, 4, P], F32, name="acc")
+            for v in range(4):
+                s = v * NQ + start
+                nc.tensor.matmul_mx(
+                    out=acc[:, v, :],
+                    lhsT=wcodes[:].bitcast(FP8X4), lhsT_scale=wscales[:],
+                    rhs=codes[:, s:s + P].bitcast(FP8X4), rhs_scale=scales[:, s:s + P],
+                    start=True, stop=True,
+                )
+            n = P - lo
+            nc.scalar.activation(
+                out=ots[k][:, q0:q0 + n, 4 * g:4 * g + 4],
+                in_=acc[:, :, lo:P].rearrange("p v q -> p q v"),
+                func=ACT.Identity, bias=bias_sb[:, 0:1], scale=1.0,
+            )
+
+        def store(k, wi):
+            start, q0, lo = WINDOWS[wi]
+            n = P - lo
+            base = (k % 4) * CH * 800
+            nc.sync.dma_start(
+                out=of[k // 4, :, base + q0 * 20:base + (q0 + n) * 20],
+                in_=ots[k][:, q0:q0 + n, :].rearrange("p q v -> p (q v)"),
+            )
+
+        def store_all(k):
+            base = (k % 4) * CH * 800
+            nc.sync.dma_start(
+                out=of[k // 4, :, base:base + NQ * 20],
+                in_=ots[k][:].rearrange("p q v -> p (q v)"),
+            )
+
+        def new_out(k):
+            ot = opool.tile([P, NQ, 20], F32, name="ot")
+            ots[k] = ot
+
+        for i in range(3):
+            load_x(i)
+        for j in range(3):
+            transposes(j)
+        park(0)
+        reload(0)
+        load_x(3)
+        load_x(4)
         wg = const.tile([P, P, 4], BF16, align_bytes=64)
         nc.vector.tensor_copy(out=wg[:], in_=raw_w[:].rearrange("p i o -> p o i"))
         wcodes = const.tile([P, P], U32, align_bytes=64)
@@ -211,11 +259,62 @@ def tile_conv2d_kernel(tc, x, weights, bias, out):
         nc.tensor.transpose(pb[:, 0, :], zb[:], ident[:])
         bias_sb = const.tile([P, 1], F32)
         nc.vector.tensor_copy(out=bias_sb[:], in_=pb[:, 0, 0:1])
-        stage_in(1)
-        copies(0, 0)
-        for i, (k, g) in enumerate(units):
-            if g == 0 and k + 2 < 8:
-                stage_in(k + 2)
-            if i + 1 < len(units):
-                copies(units[i + 1][0], units[i + 1][1])
-            compute(k, g)
+        for j in range(3, 6):
+            transposes(j)
+        park(1)
+        reload(1)
+        for i in range(5, 9):
+            load_x(i)
+
+        units = [(k, g) for k in range(NK) for g in range(5)]
+        n_plain = 5 * (NK - 1)
+        st = {"groups": 6, "out": 6, "parks": 2, "reloads": 2, "copied": 0}
+
+        def try_reload():
+            r = st["reloads"]
+            if r < NK and st["parks"] > r and st["copied"] >= 5 * (r - XR_BUFS + 1):
+                reload(r)
+                st["reloads"] += 1
+
+        def copy_ahead(upto):
+            while st["copied"] <= min(upto, len(units) - 1):
+                kk, gg = units[st["copied"]]
+                copies(kk, gg)
+                st["copied"] += 1
+                try_reload()
+
+        copy_ahead(LOOK - 1)
+        for i in range(n_plain):
+            k, g = units[i]
+            copy_ahead(i + LOOK)
+            if g == 0:
+                new_out(k)
+            new_codes(k, g)
+            quantise(k, g, 0, 1024)
+            quantise(k, g, 1024, 1280)
+            if st["groups"] > st["out"]:
+                transposes_out(st["out"])
+                st["out"] += 1
+                while st["parks"] < NK and (CL * (st["parks"] + 1) - 1) // P < 4 * st["out"]:
+                    park(st["parks"])
+                    st["parks"] += 1
+                try_reload()
+            for wi in range(3):
+                passes(k, g, wi)
+            if g == 4:
+                store_all(k)
+            if st["groups"] < NG:
+                transposes_pe(st["groups"])
+                st["groups"] += 1
+
+        k = NK - 1
+        copy_ahead(len(units) - 1)
+        new_out(k)
+        for g in range(5):
+            new_codes(k, g)
+        for wi, (w0, w1) in enumerate(((0, 128), (128, 256), (256, 320))):
+            for g in range(5):
+                for v in range(4):
+                    quantise(k, g, v * NQ + w0, v * NQ + w1)
+                passes(k, g, wi)
+            store(k, wi)

@@ -25,7 +25,7 @@ CW = CL // 2
 NQ = CH * 40
 HI0 = 35
 PIECES = ((0, 12), (12, 24), (24, 32), (32, 44), (44, 52), (52, 64), (64, 72), (72, 81), (81, 82))
-S_SHARE = ((0, 1, 2), (0, 1, 2), (0, 1, 2), (0, 1, 2), (0, 1))
+S_SHARE = ((0, 1), (0, 1), (0, 1), (0, 1), (0, 1))
 LOOK = 2
 XR_BUFS = 2
 WINDOWS = ((0, 0, 0), (128, 128, 0), (192, 256, 64))

@@ -24,8 +24,7 @@ CLP = 1312
 CW = CL // 2
 NQ = CH * 40
 HI0 = 35
-PIECES = ((0, 12), (12, 24), (24, 32), (32, 44), (44, 52), (52, 64), (64, 72), (72, 81), (81, 82))
-S_SHARE = ((0, 1), (0, 1), (0, 1), (0, 1), (0, 1))
+S_SHARE = ((0, 1, 2), (0, 1), (0, 1, 2), (0, 1), (0, 1))
 LOOK = 2
 XR_BUFS = 2
 WINDOWS = ((0, 0, 0), (128, 128, 0), (192, 256, 64))
@@ -58,16 +57,17 @@ def tile_conv2d_kernel(tc, x, weights, bias, out):
 
         x_of_tile = {}
 
-        def load_x(i):
-            t0, t1 = PIECES[i]
-            xp = const.tile([P, t1 - t0, HW], BF16, name="xp%d" % i)
-            r0 = min(P * t0, ROWS - P)
-            nc.sync.dma_start(
-                out=xp[:],
-                in_=x_rows[r0:r0 + P * (t1 - t0), :].rearrange("(t p) w -> p t w", p=P),
-            )
-            for t in range(t0, t1):
-                x_of_tile[t] = (xp, t - t0)
+        def load_x(j):
+            spans = [(4 * j, 4 * j + 4)] if j < NG - 1 else [(80, 81), (81, 82)]
+            for (t0, t1) in spans:
+                xp = const.tile([P, t1 - t0, HW], BF16, name="xp%d" % t0)
+                r0 = min(P * t0, ROWS - P)
+                nc.sync.dma_start(
+                    out=xp[:],
+                    in_=x_rows[r0:r0 + P * (t1 - t0), :].rearrange("(t p) w -> p t w", p=P),
+                )
+                for t in range(t0, t1):
+                    x_of_tile[t] = (xp, t - t0)
 
         xt_lo = const.tile([P, ROWS], BF16)
         xt_hi = const.tile([P, ROWS], BF16)
@@ -239,14 +239,20 @@ def tile_conv2d_kernel(tc, x, weights, bias, out):
             ot = opool.tile([P, NQ, 20], F32, name="ot")
             ots[k] = ot
 
-        for i in range(3):
-            load_x(i)
+        for j in range(8):
+            load_x(j)
         for j in range(3):
             transposes(j)
         park(0)
+        for j in range(8, 12):
+            load_x(j)
         reload(0)
-        load_x(3)
-        load_x(4)
+        for j in range(3, 6):
+            transposes(j)
+        park(1)
+        for j in range(12, 16):
+            load_x(j)
+        reload(1)
         wg = const.tile([P, P, 4], BF16, align_bytes=64)
         nc.vector.tensor_copy(out=wg[:], in_=raw_w[:].rearrange("p i o -> p o i"))
         wcodes = const.tile([P, P], U32, align_bytes=64)
@@ -259,16 +265,15 @@ def tile_conv2d_kernel(tc, x, weights, bias, out):
         nc.tensor.transpose(pb[:, 0, :], zb[:], ident[:])
         bias_sb = const.tile([P, 1], F32)
         nc.vector.tensor_copy(out=bias_sb[:], in_=pb[:, 0, 0:1])
-        for j in range(3, 6):
+        for j in range(6, 8):
             transposes(j)
-        park(1)
-        reload(1)
-        for i in range(5, 9):
-            load_x(i)
+        park(2)
+        for j in range(16, NG):
+            load_x(j)
 
         units = [(k, g) for k in range(NK) for g in range(5)]
         n_plain = 5 * (NK - 1)
-        st = {"groups": 6, "out": 6, "parks": 2, "reloads": 2, "copied": 0}
+        st = {"groups": 8, "out": 8, "parks": 3, "reloads": 2, "copied": 0}
 
         def try_reload():
             r = st["reloads"]

@@ -9,6 +9,8 @@ U32 = mybir.dt.uint32
 U8 = mybir.dt.uint8
 FP8X4 = mybir.dt.float8_e4m3fn_x4
 ACT = mybir.ActivationFunctionType
+ALU = mybir.AluOpType
+I32 = mybir.dt.int32
 
 FLOPS = 2 * 51200 * 512 * 128
 
@@ -24,7 +26,11 @@ CLP = 1312
 CW = CL // 2
 NQ = CH * 40
 HI0 = 35
-S_SHARE = ((0, 1, 2), (0, 1), (0, 1, 2), (0, 1), (0, 1))
+XPITCH = 176
+ROW0 = (0, 32, 64, 96 - HI0, 128 - HI0)
+XT_UNITS = (3, 17)
+SHARE_XT = (2, 2, 2, 2, 1)
+SHARE = (2, 3, 2, 3, 2)
 LOOK = 2
 XR_BUFS = 2
 WINDOWS = ((0, 0, 0), (128, 128, 0), (192, 256, 64))
@@ -60,10 +66,10 @@ def tile_conv2d_kernel(tc, x, weights, bias, out):
         def load_x(j):
             spans = [(4 * j, 4 * j + 4)] if j < NG - 1 else [(80, 81), (81, 82)]
             for (t0, t1) in spans:
-                xp = const.tile([P, t1 - t0, HW], BF16, name="xp%d" % t0)
+                xp = const.tile([P, t1 - t0, XPITCH], BF16, name="xp%d" % t0)
                 r0 = min(P * t0, ROWS - P)
                 nc.sync.dma_start(
-                    out=xp[:],
+                    out=xp[:, :, 0:HW],
                     in_=x_rows[r0:r0 + P * (t1 - t0), :].rearrange("(t p) w -> p t w", p=P),
                 )
                 for t in range(t0, t1):
@@ -74,77 +80,74 @@ def tile_conv2d_kernel(tc, x, weights, bias, out):
         xt = [xt_lo, xt_hi]
         w0s = [0, HI0]
 
-        def evac(gi, dst, src):
-            if gi == 0:
+        def evac(eng, dst, src):
+            if eng == 0:
                 nc.vector.tensor_copy(out=dst, in_=src)
             else:
                 nc.scalar.copy(out=dst, in_=src)
 
         pending = {}
 
-        def transposes_pe(j):
+        def transposes_pe(j, gi):
             tg0 = 4 * j
-            n = min(4, NT - tg0)
-            pts = []
-            for gi in range(2):
-                pt = psum_t.tile([P, 4, P], BF16, name="pt")
-                for u in range(n):
-                    xp, tl = x_of_tile[tg0 + u]
-                    nc.tensor.transpose(pt[:, u, :], xp[:, tl, w0s[gi]:w0s[gi] + P], ident[:])
-                pts.append(pt)
-            pending[j] = pts
+            pt = psum_t.tile([P, 4, P], BF16, name="pt")
+            for u in range(min(4, NT - tg0)):
+                xp, tl = x_of_tile[tg0 + u]
+                nc.tensor.transpose(pt[:, u, :], xp[:, tl, w0s[gi]:w0s[gi] + P], ident[:])
+            pending[(j, gi)] = pt
 
-        def transposes(j):
-            transposes_pe(j)
-            transposes_out(j)
-
-        def transposes_out(j):
+        def transposes_out(j, gi, eng):
             tg0 = 4 * j
-            n = min(4, NT - tg0)
-            pts = pending[j]
-            for gi in range(2):
-                pt = pts[gi]
-                if n == 4:
-                    evac(gi, xt[gi][:, P * tg0:P * tg0 + 4 * P],
-                         pt[:].rearrange("p u r -> p (u r)"))
-                else:
-                    evac(gi, xt[gi][:, P * tg0:P * tg0 + P], pt[:, 0, :])
-                    evac(gi, xt[gi][:, P * tg0 + P:ROWS], pt[:, 1, 64:P])
+            pt = pending[(j, gi)]
+            if NT - tg0 >= 4:
+                evac(eng, xt[gi][:, P * tg0:P * tg0 + 4 * P], pt[:].rearrange("p u r -> p (u r)"))
+            else:
+                evac(eng, xt[gi][:, P * tg0:P * tg0 + P], pt[:, 0, :])
+                evac(eng, xt[gi][:, P * tg0 + P:ROWS], pt[:, 1, 64:P])
 
         def slot(k, gi):
             if k >= 4:
                 return 19200 + ((k - 4) * 2 + gi) * CW
             return 12800 + (k * 2 + gi) * CW
 
+        def park_half(k, gi):
+            col = slot(k, gi)
+            nc.sync.dma_start(
+                out=of[1, :, col:col + CW],
+                in_=xt[gi][:, CL * k:CL * (k + 1)].bitcast(F32),
+            )
+
         def park(k):
-            for gi in range(2):
-                col = slot(k, gi)
-                nc.sync.dma_start(
-                    out=of[1, :, col:col + CW],
-                    in_=xt[gi][:, CL * k:CL * (k + 1)].bitcast(F32),
-                )
+            park_half(k, 0)
+            park_half(k, 1)
 
         xrs = {}
         ots = {}
         tgs = {}
         cds = {}
 
-        def reload(k):
-            xr = reppool.tile([P, 5, CLP], BF16, name="xr")
-            xr32 = xr[:].bitcast(F32)
+        def reload_half(k, gi):
+            if gi == 0:
+                xr_new = reppool.tile([P, 5, CLP], BF16, name="xr")
+                xrs[k] = xr_new
+            xr32 = xrs[k][:].bitcast(F32)
+            col = slot(k, gi)
             for dj in range(4):
-                col = slot(k, 0)
-                nc.sync.dma_start(
-                    out=xr32[dj:P:4, 0:3, 0:CW],
-                    in_=of[1, dj:dj + 96, col:col + CW].rearrange("(j m) c -> m j c", m=32),
-                )
-                col = slot(k, 1)
-                r0 = 96 - HI0 + dj
-                nc.sync.dma_start(
-                    out=xr32[dj:P:4, 3:5, 0:CW],
-                    in_=of[1, r0:r0 + 64, col:col + CW].rearrange("(j m) c -> m j c", m=32),
-                )
-            xrs[k] = xr
+                if gi == 0:
+                    nc.sync.dma_start(
+                        out=xr32[dj:P:4, 0:3, 0:CW],
+                        in_=of[1, dj:dj + 96, col:col + CW].rearrange("(j m) c -> m j c", m=32),
+                    )
+                else:
+                    r0 = 96 - HI0 + dj
+                    nc.sync.dma_start(
+                        out=xr32[dj:P:4, 3:5, 0:CW],
+                        in_=of[1, r0:r0 + 64, col:col + CW].rearrange("(j m) c -> m j c", m=32),
+                    )
+
+        def reload(k):
+            reload_half(k, 0)
+            reload_half(k, 1)
 
         def copies(k, g):
             xr = xrs[k]
@@ -155,13 +158,14 @@ def tile_conv2d_kernel(tc, x, weights, bias, out):
             tg5 = tg[:].rearrange("p v (c e h) -> p v c e h", e=2, h=160)
             tw = tg[:].bitcast(F32).rearrange("p v (c e w) -> p v c e w", e=2, w=80)
             tg4 = tg[:].rearrange("p v (c h) -> p v c h", h=160)
+            n_shared = SHARE_XT[g] if XT_UNITS[0] <= 5 * k + g <= XT_UNITS[1] else SHARE[g]
             runs = []
             a = 0
             while a < 4:
                 phi, jb0 = divmod(4 * g + a, 5)
-                shared = a in S_SHARE[g]
+                shared = a < n_shared
                 n = 1
-                while (a + n < 4 and jb0 + n < 5 and ((a + n) in S_SHARE[g]) == shared):
+                while (a + n < 4 and jb0 + n < 5 and (a + n < n_shared) == shared):
                     n += 1
                 runs.append((a, n, phi, jb0, shared))
                 a += n
@@ -239,20 +243,49 @@ def tile_conv2d_kernel(tc, x, weights, bias, out):
             ot = opool.tile([P, NQ, 20], F32, name="ot")
             ots[k] = ot
 
+        def stage_groups(j0, j1):
+            for j in range(j0, j1):
+                for gi in range(2):
+                    transposes_pe(j, gi)
+                for gi in range(2):
+                    transposes_out(j, gi, gi)
+
+        diff = const.tile([P, P], I32)
+        nc.gpsimd.iota(diff[:], pattern=[[1, 32], [1, 4]], base=0, channel_multiplier=-1)
+        sels = []
+        for jb in range(5):
+            sel = const.tile([P, P], BF16, name="sel%d" % jb)
+            nc.vector.tensor_scalar(
+                out=sel[:], in0=diff[:], scalar1=float(-ROW0[jb]), scalar2=None, op0=ALU.is_equal,
+            )
+            sels.append(sel)
+
         for j in range(8):
             load_x(j)
-        for j in range(3):
-            transposes(j)
-        park(0)
+        stage_groups(0, 3)
         for j in range(8, 12):
             load_x(j)
-        reload(0)
-        for j in range(3, 6):
-            transposes(j)
+
+        xr_first = reppool.tile([P, 5, CLP], BF16, name="xr")
+        xrs[0] = xr_first
+        for jb in range(5):
+            src = xt[0] if jb < 3 else xt[1]
+            bank_a = psum_m.tile([P, 1024], BF16, name="acc")
+            bank_b = psum_m.tile([P, 1024], BF16, name="acc")
+            for (c0, n, bank, b0) in ((0, 512, bank_a, 0), (512, 512, bank_a, 512),
+                                      (1024, 256, bank_b, 0), (1280, 32, bank_b, 256)):
+                nc.tensor.matmul(
+                    out=bank[:, b0:b0 + n], lhsT=sels[jb][:], rhs=src[:, c0:c0 + n],
+                    start=True, stop=True,
+                )
+            evac(jb % 2, xr_first[:, jb, 0:1024], bank_a[:])
+            evac(1 - jb % 2, xr_first[:, jb, 1024:CL], bank_b[:, 0:CL - 1024])
+
+        stage_groups(3, 6)
         park(1)
-        for j in range(12, 16):
-            load_x(j)
         reload(1)
+        for j in range(12, NG):
+            load_x(j)
         wg = const.tile([P, P, 4], BF16, align_bytes=64)
         nc.vector.tensor_copy(out=wg[:], in_=raw_w[:].rearrange("p i o -> p o i"))
         wcodes = const.tile([P, P], U32, align_bytes=64)
@@ -265,15 +298,10 @@ def tile_conv2d_kernel(tc, x, weights, bias, out):
         nc.tensor.transpose(pb[:, 0, :], zb[:], ident[:])
         bias_sb = const.tile([P, 1], F32)
         nc.vector.tensor_copy(out=bias_sb[:], in_=pb[:, 0, 0:1])
-        for j in range(6, 8):
-            transposes(j)
-        park(2)
-        for j in range(16, NG):
-            load_x(j)
 
         units = [(k, g) for k in range(NK) for g in range(5)]
         n_plain = 5 * (NK - 1)
-        st = {"groups": 8, "out": 8, "parks": 3, "reloads": 2, "copied": 0}
+        st = {"groups": 6, "out": 6, "parks": 2, "reloads": 2, "copied": 0}
 
         def try_reload():
             r = st["reloads"]
@@ -298,7 +326,8 @@ def tile_conv2d_kernel(tc, x, weights, bias, out):
             quantise(k, g, 0, 1024)
             quantise(k, g, 1024, 1280)
             if st["groups"] > st["out"]:
-                transposes_out(st["out"])
+                transposes_out(st["out"], 0, 1)
+                transposes_out(st["out"], 1, 1)
                 st["out"] += 1
                 while st["parks"] < NK and (CL * (st["parks"] + 1) - 1) // P < 4 * st["out"]:
                     park(st["parks"])
@@ -309,7 +338,8 @@ def tile_conv2d_kernel(tc, x, weights, bias, out):
             if g == 4:
                 store_all(k)
             if st["groups"] < NG:
-                transposes_pe(st["groups"])
+                transposes_pe(st["groups"], 0)
+                transposes_pe(st["groups"], 1)
                 st["groups"] += 1
 
         k = NK - 1

@@ -32,6 +32,7 @@ XT_UNITS = (3, 17)
 SHARE_XT = (2, 2, 2, 2, 1)
 SHARE = (2, 3, 2, 3, 2)
 LOOK = 2
+FIRST = 4
 XR_BUFS = 2
 WINDOWS = ((0, 0, 0), (128, 128, 0), (192, 256, 64))
 
@@ -149,12 +150,15 @@ def tile_conv2d_kernel(tc, x, weights, bias, out):
             reload_half(k, 0)
             reload_half(k, 1)
 
-        def copies(k, g):
+        def copies(k, g, part=None):
             xr = xrs[k]
             xr5 = xr[:, :, 0:CL].rearrange("p j (c e h) -> p j c e h", e=2, h=HW)
             xw = xr[:].bitcast(F32)[:, :, 0:CW].rearrange("p j (c w) -> p j c w", w=HW)
             xr4 = xr[:, :, 0:CL].rearrange("p j (c h) -> p j c h", h=HW)
-            tg = tpool.tile([P, 4, 4 * NQ], BF16, align_bytes=64, name="tg")
+            if part != 1:
+                tg_new = tpool.tile([P, 4, 4 * NQ], BF16, align_bytes=64, name="tg")
+                tgs[(k, g)] = tg_new
+            tg = tgs[(k, g)]
             tg5 = tg[:].rearrange("p v (c e h) -> p v c e h", e=2, h=160)
             tw = tg[:].bitcast(F32).rearrange("p v (c e w) -> p v c e w", e=2, w=80)
             tg4 = tg[:].rearrange("p v (c h) -> p v c h", h=160)
@@ -165,9 +169,11 @@ def tile_conv2d_kernel(tc, x, weights, bias, out):
                 phi, jb0 = divmod(4 * g + a, 5)
                 shared = a < n_shared
                 n = 1
-                while (a + n < 4 and jb0 + n < 5 and (a + n < n_shared) == shared):
+                while (a + n < 4 and jb0 + n < 5 and (a + n < n_shared) == shared
+                       and (part is None or (jb0 + n < 3) == (jb0 < 3))):
                     n += 1
-                runs.append((a, n, phi, jb0, shared))
+                if part is None or (jb0 >= 3) == (part == 1):
+                    runs.append((a, n, phi, jb0, shared))
                 a += n
             for (a, n, phi, jb0, shared) in runs:
                 if shared:
@@ -189,7 +195,6 @@ def tile_conv2d_kernel(tc, x, weights, bias, out):
                         out=tw[:, a:a + n, :, par, :],
                         in_=xw[:, jb0:jb0 + n, :, s0:s0 + 80],
                     )
-            tgs[(k, g)] = tg
 
         def new_codes(k, g):
             codes = cpool.tile([P, 4 * NQ], U32, align_bytes=64, name="codes")
@@ -262,13 +267,22 @@ def tile_conv2d_kernel(tc, x, weights, bias, out):
 
         for j in range(8):
             load_x(j)
+        wg = const.tile([P, P, 4], BF16, align_bytes=64)
+        nc.vector.tensor_copy(out=wg[:], in_=raw_w[:].rearrange("p i o -> p o i"))
+        wcodes = const.tile([P, P], U32, align_bytes=64)
+        wscales = const.tile([P, P], U8, align_bytes=64)
+        nc.vector.quantize_mx(
+            out=wcodes[:].bitcast(FP8X4), scales=wscales[:],
+            in_=wg[:].rearrange("p o i -> p (o i)"),
+        )
         stage_groups(0, 3)
         for j in range(8, 12):
             load_x(j)
 
         xr_first = reppool.tile([P, 5, CLP], BF16, name="xr")
         xrs[0] = xr_first
-        for jb in range(5):
+
+        def spread(jb):
             src = xt[0] if jb < 3 else xt[1]
             bank_a = psum_m.tile([P, 1024], BF16, name="acc")
             bank_b = psum_m.tile([P, 1024], BF16, name="acc")
@@ -278,30 +292,34 @@ def tile_conv2d_kernel(tc, x, weights, bias, out):
                     out=bank[:, b0:b0 + n], lhsT=sels[jb][:], rhs=src[:, c0:c0 + n],
                     start=True, stop=True,
                 )
-            evac(jb % 2, xr_first[:, jb, 0:1024], bank_a[:])
-            evac(1 - jb % 2, xr_first[:, jb, 1024:CL], bank_b[:, 0:CL - 1024])
+            evac(jb % 2 if jb < 3 else 1, xr_first[:, jb, 0:1024], bank_a[:])
+            evac(1 - jb % 2 if jb < 3 else 1, xr_first[:, jb, 1024:CL], bank_b[:, 0:CL - 1024])
 
-        stage_groups(3, 6)
+        for jb in range(3):
+            spread(jb)
+        for j in range(3, 6):
+            for gi in range(2):
+                transposes_pe(j, gi)
+            for gi in range(2):
+                transposes_out(j, gi, 1)
         park(1)
         reload(1)
         for j in range(12, NG):
             load_x(j)
-        wg = const.tile([P, P, 4], BF16, align_bytes=64)
-        nc.vector.tensor_copy(out=wg[:], in_=raw_w[:].rearrange("p i o -> p o i"))
-        wcodes = const.tile([P, P], U32, align_bytes=64)
-        wscales = const.tile([P, P], U8, align_bytes=64)
-        nc.vector.quantize_mx(
-            out=wcodes[:].bitcast(FP8X4), scales=wscales[:],
-            in_=wg[:].rearrange("p o i -> p (o i)"),
-        )
+        for jb in range(3, 5):
+            spread(jb)
+        for g in range(FIRST):
+            copies(0, g, 0)
         pb = psum_t.tile([P, 4, P], BF16, name="pt")
         nc.tensor.transpose(pb[:, 0, :], zb[:], ident[:])
         bias_sb = const.tile([P, 1], F32)
         nc.vector.tensor_copy(out=bias_sb[:], in_=pb[:, 0, 0:1])
+        for g in range(FIRST):
+            copies(0, g, 1)
 
         units = [(k, g) for k in range(NK) for g in range(5)]
         n_plain = 5 * (NK - 1)
-        st = {"groups": 6, "out": 6, "parks": 2, "reloads": 2, "copied": 0}
+        st = {"groups": 6, "out": 6, "parks": 2, "reloads": 2, "copied": FIRST}
 
         def try_reload():
             r = st["reloads"]

@@ -7,10 +7,10 @@ BF16 = mybir.dt.bfloat16
 F32 = mybir.dt.float32
 U32 = mybir.dt.uint32
 U8 = mybir.dt.uint8
+I32 = mybir.dt.int32
 FP8X4 = mybir.dt.float8_e4m3fn_x4
 ACT = mybir.ActivationFunctionType
 ALU = mybir.AluOpType
-I32 = mybir.dt.int32
 
 FLOPS = 2 * 51200 * 512 * 128
 
@@ -19,35 +19,44 @@ HW = 163
 ROWS = 64 * HW
 NT = 82
 NG = 21
-CH = 8
-NK = 8
-CL = CH * HW
-CLP = 1312
-CW = CL // 2
-NQ = CH * 40
+GF = 512
 HI0 = 35
 XPITCH = 176
 ROW0 = (0, 32, 64, 96 - HI0, 128 - HI0)
-XT_UNITS = (3, 17)
-SHARE_XT = (2, 2, 2, 2, 1)
-SHARE = (2, 3, 2, 3, 2)
-LOOK = 2
-FIRST = 4
-XR_BUFS = 2
-WINDOWS = ((0, 0, 0), (128, 128, 0), (192, 256, 64))
+CHUNK_WORDS = (128,) + (256,) * 9 + (128, 64)
+NMAX = 256
+XRP = 4 * NMAX + 32
+WIN = 128
+RW = 6
+WF = 20 * WIN
+RINGF = RW * WF
+CPITCH = 5 * HW
+PKP = 5256
+PK0 = 25600 - 2 * PKP
+NPE = 2
+XR_BUFS = 3
+S2_EARLY, S2_LATE = 4, 5
+TENG = (0, 1) + (1,) * 19
+TSTEPS = 3
+QW = (1024, 512, 256, 128, 64, 32)
 
 
 def tile_conv2d_kernel(tc, x, weights, bias, out):
     nc = tc.nc
     x_rows = x.rearrange("b c h w -> (b c h) w")
     of = out.rearrange("b o u v -> b o (u v)")
+    chunks = []
+    for n in CHUNK_WORDS:
+        chunks.append((sum(c[1] for c in chunks), n))
+    NC = len(chunks)
 
     with ExitStack() as ctx:
         const = ctx.enter_context(tc.tile_pool(name="const", bufs=1))
-        reppool = ctx.enter_context(tc.tile_pool(name="rep", bufs=XR_BUFS))
-        tpool = ctx.enter_context(tc.tile_pool(name="tp", bufs=5))
-        cpool = ctx.enter_context(tc.tile_pool(name="cp", bufs=5))
-        opool = ctx.enter_context(tc.tile_pool(name="op", bufs=2))
+        xtpool = ctx.enter_context(tc.tile_pool(name="xt", bufs=3))
+        xrpool = ctx.enter_context(tc.tile_pool(name="rep", bufs=XR_BUFS))
+        xspool = ctx.enter_context(tc.tile_pool(name="xs", bufs=2))
+        x2pool = ctx.enter_context(tc.tile_pool(name="xs2", bufs=2))
+        cpool = ctx.enter_context(tc.tile_pool(name="cp", bufs=7))
         psum_t = ctx.enter_context(tc.psum_pool(name="pst", bufs=2))
         psum_m = ctx.enter_context(tc.psum_pool(name="psm", bufs=6))
         ctx.enter_context(tc.manual_schedule())
@@ -61,6 +70,7 @@ def tile_conv2d_kernel(tc, x, weights, bias, out):
         w_view = weights.rearrange("(m i j) o -> j m i o", i=4, j=4)
         for dj in range(4):
             nc.scalar.dma_start(out=raw_w[dj:P:4, :, :], in_=w_view[dj])
+        ring = const.tile([P, RINGF + 16], F32)
 
         x_of_tile = {}
 
@@ -76,11 +86,6 @@ def tile_conv2d_kernel(tc, x, weights, bias, out):
                 for t in range(t0, t1):
                     x_of_tile[t] = (xp, t - t0)
 
-        xt_lo = const.tile([P, ROWS], BF16)
-        xt_hi = const.tile([P, ROWS], BF16)
-        xt = [xt_lo, xt_hi]
-        w0s = [0, HI0]
-
         def evac(eng, dst, src):
             if eng == 0:
                 nc.vector.tensor_copy(out=dst, in_=src)
@@ -88,172 +93,179 @@ def tile_conv2d_kernel(tc, x, weights, bias, out):
                 nc.scalar.copy(out=dst, in_=src)
 
         pending = {}
-
-        def transposes_pe(j, gi):
-            tg0 = 4 * j
-            pt = psum_t.tile([P, 4, P], BF16, name="pt")
-            for u in range(min(4, NT - tg0)):
-                xp, tl = x_of_tile[tg0 + u]
-                nc.tensor.transpose(pt[:, u, :], xp[:, tl, w0s[gi]:w0s[gi] + P], ident[:])
-            pending[(j, gi)] = pt
-
-        def transposes_out(j, gi, eng):
-            tg0 = 4 * j
-            pt = pending[(j, gi)]
-            if NT - tg0 >= 4:
-                evac(eng, xt[gi][:, P * tg0:P * tg0 + 4 * P], pt[:].rearrange("p u r -> p (u r)"))
-            else:
-                evac(eng, xt[gi][:, P * tg0:P * tg0 + P], pt[:, 0, :])
-                evac(eng, xt[gi][:, P * tg0 + P:ROWS], pt[:, 1, 64:P])
-
-        def slot(k, gi):
-            if k >= 4:
-                return 19200 + ((k - 4) * 2 + gi) * CW
-            return 12800 + (k * 2 + gi) * CW
-
-        def park_half(k, gi):
-            col = slot(k, gi)
-            nc.sync.dma_start(
-                out=of[1, :, col:col + CW],
-                in_=xt[gi][:, CL * k:CL * (k + 1)].bitcast(F32),
-            )
-
-        def park(k):
-            park_half(k, 0)
-            park_half(k, 1)
-
+        xbs = {}
         xrs = {}
-        ots = {}
-        tgs = {}
+        xss = {}
         cds = {}
 
-        def reload_half(k, gi):
-            if gi == 0:
-                xr_new = reppool.tile([P, 5, CLP], BF16, name="xr")
-                xrs[k] = xr_new
-            xr32 = xrs[k][:].bitcast(F32)
-            col = slot(k, gi)
-            for dj in range(4):
-                if gi == 0:
+        def transposes_pe(j):
+            pt = psum_t.tile([P, 2, 4, P], BF16, name="pt")
+            for gi in range(2):
+                for u in range(min(4, NT - 4 * j)):
+                    xp, tl = x_of_tile[4 * j + u]
+                    nc.tensor.transpose(pt[:, gi, u, :], xp[:, tl, gi * HI0:gi * HI0 + P], ident[:])
+            pending[j] = pt
+
+        def transposes_out(j, eng):
+            if j % 2 == 0:
+                xb_new = xtpool.tile([P, 2, 2, GF], BF16, name="xb")
+                xbs[j // 2] = xb_new
+            xb = xbs[j // 2]
+            pt = pending[j]
+            if j < NG - 1:
+                evac(eng, xb[:, j % 2, :, :], pt[:].rearrange("p g u r -> p g (u r)"))
+            else:
+                nc.gpsimd.memset(xb[:, 0, :, 192:272], 0.0)
+                evac(eng, xb[:, 0, :, 0:P], pt[:, :, 0, :])
+                evac(eng, xb[:, 0, :, P:192], pt[:, :, 1, 64:P])
+
+        def group(j, gi, n):
+            return xbs[j // 2][:, j % 2, gi, 0:n]
+
+        def park(tb):
+            for gi in range(2):
+                col = PK0 + gi * PKP + GF * tb
+                if tb < NG // 2:
                     nc.sync.dma_start(
-                        out=xr32[dj:P:4, 0:3, 0:CW],
-                        in_=of[1, dj:dj + 96, col:col + CW].rearrange("(j m) c -> m j c", m=32),
+                        out=of[1, :, col:col + GF].rearrange("o (h c) -> o h c", h=2),
+                        in_=xbs[tb][:, :, gi, :].bitcast(F32),
                     )
                 else:
-                    r0 = 96 - HI0 + dj
+                    nc.sync.dma_start(out=of[1, :, col:col + 136], in_=xbs[tb][:, 0, gi, 0:272].bitcast(F32))
+
+        def new_xr(c):
+            xr = xrpool.tile([P, 5, XRP], BF16, align_bytes=64, name="xr")
+            xrs[c] = xr
+            return xr
+
+        def reload(c):
+            w0, n = chunks[c]
+            xr32 = new_xr(c)[:].bitcast(F32)
+            ln = 2 * n + 2
+            for gi, (j0, j1, r0) in enumerate(((0, 3, 0), (3, 5, 96 - HI0))):
+                col = PK0 + gi * PKP + 2 * w0
+                for dj in range(4):
                     nc.sync.dma_start(
-                        out=xr32[dj:P:4, 3:5, 0:CW],
-                        in_=of[1, r0:r0 + 64, col:col + CW].rearrange("(j m) c -> m j c", m=32),
+                        out=xr32[dj:P:4, j0:j1, 0:ln],
+                        in_=of[1, r0 + dj:r0 + dj + 32 * (j1 - j0), col:col + ln].rearrange("(j m) c -> m j c", m=32),
                     )
 
-        def reload(k):
-            reload_half(k, 0)
-            reload_half(k, 1)
-
-        def copies(k, g, part=None):
-            xr = xrs[k]
-            xr5 = xr[:, :, 0:CL].rearrange("p j (c e h) -> p j c e h", e=2, h=HW)
-            xw = xr[:].bitcast(F32)[:, :, 0:CW].rearrange("p j (c w) -> p j c w", w=HW)
-            xr4 = xr[:, :, 0:CL].rearrange("p j (c h) -> p j c h", h=HW)
-            if part != 1:
-                tg_new = tpool.tile([P, 4, 4 * NQ], BF16, align_bytes=64, name="tg")
-                tgs[(k, g)] = tg_new
-            tg = tgs[(k, g)]
-            tg5 = tg[:].rearrange("p v (c e h) -> p v c e h", e=2, h=160)
-            tw = tg[:].bitcast(F32).rearrange("p v (c e w) -> p v c e w", e=2, w=80)
-            tg4 = tg[:].rearrange("p v (c h) -> p v c h", h=160)
-            n_shared = SHARE_XT[g] if XT_UNITS[0] <= 5 * k + g <= XT_UNITS[1] else SHARE[g]
-            runs = []
-            a = 0
-            while a < 4:
-                phi, jb0 = divmod(4 * g + a, 5)
-                shared = a < n_shared
-                n = 1
-                while (a + n < 4 and jb0 + n < 5 and (a + n < n_shared) == shared
-                       and (part is None or (jb0 + n < 3) == (jb0 < 3))):
-                    n += 1
-                if part is None or (jb0 >= 3) == (part == 1):
-                    runs.append((a, n, phi, jb0, shared))
-                a += n
-            for (a, n, phi, jb0, shared) in runs:
-                if shared:
-                    par = phi % 2
-                    nc.vector.tensor_copy(
-                        out=tg5[:, a:a + n, :, 1 - par, :],
-                        in_=xr5[:, jb0:jb0 + n, :, 1 - par, phi:phi + 160],
+        def spread(c, engs):
+            w0, n = chunks[c]
+            f0, ln = 4 * w0, 4 * n
+            xr = new_xr(c)
+            over = psum_m.tile([P, 1024], BF16, name="acc")
+            for jb in range(5):
+                gi = 0 if jb < 3 else 1
+                bank = psum_m.tile([P, 1024], BF16, name="acc")
+                for q in range(ln // GF):
+                    nc.tensor.matmul(
+                        out=bank[:, GF * q:GF * (q + 1)], lhsT=sels[jb][:], rhs=group(f0 // GF + q, gi, GF),
+                        start=True, stop=True,
                     )
-                else:
-                    nc.vector.tensor_copy(
-                        out=tg4[:, a:a + n, :, :],
-                        in_=xr4[:, jb0:jb0 + n, :, phi:phi + 160],
-                    )
-            for (a, n, phi, jb0, shared) in runs:
-                if shared:
-                    par = phi % 2
-                    s0 = (par * HW + phi) // 2
-                    nc.scalar.copy(
-                        out=tw[:, a:a + n, :, par, :],
-                        in_=xw[:, jb0:jb0 + n, :, s0:s0 + 80],
-                    )
-
-        def new_codes(k, g):
-            codes = cpool.tile([P, 4 * NQ], U32, align_bytes=64, name="codes")
-            scales = cpool.tile([P, 4 * NQ], U8, align_bytes=64, name="scales")
-            cds[(k, g)] = (codes, scales)
-
-        def quantise(k, g, w0, w1):
-            codes, scales = cds[(k, g)]
-            tflat = tgs[(k, g)][:].rearrange("p v e -> p (v e)")
-            nc.vector.quantize_mx(
-                out=codes[:, w0:w1].bitcast(FP8X4), scales=scales[:, w0:w1],
-                in_=tflat[:, 4 * w0:4 * w1],
-            )
-
-        def passes(k, g, wi):
-            start, q0, lo = WINDOWS[wi]
-            codes, scales = cds[(k, g)]
-            acc = psum_m.tile([P, 4, P], F32, name="acc")
-            for v in range(4):
-                s = v * NQ + start
-                nc.tensor.matmul_mx(
-                    out=acc[:, v, :],
-                    lhsT=wcodes[:].bitcast(FP8X4), lhsT_scale=wscales[:],
-                    rhs=codes[:, s:s + P].bitcast(FP8X4), rhs_scale=scales[:, s:s + P],
+                nc.tensor.matmul(
+                    out=over[:, 4 * jb:4 * jb + 4], lhsT=sels[jb][:], rhs=group((f0 + ln) // GF, gi, 4),
                     start=True, stop=True,
                 )
-            n = P - lo
-            nc.scalar.activation(
-                out=ots[k][:, q0:q0 + n, 4 * g:4 * g + 4],
-                in_=acc[:, :, lo:P].rearrange("p v q -> p q v"),
-                func=ACT.Identity, bias=bias_sb[:, 0:1], scale=1.0,
-            )
+                evac(engs[jb], xr[:, jb, 0:ln], bank[:, 0:ln])
+            evac(engs[5], xr[:, :, ln:ln + 4], over[:, 0:20].rearrange("p (j e) -> p j e", e=4))
 
-        def store(k, wi):
-            start, q0, lo = WINDOWS[wi]
-            n = P - lo
-            base = (k % 4) * CH * 800
-            nc.sync.dma_start(
-                out=of[k // 4, :, base + q0 * 20:base + (q0 + n) * 20],
-                in_=ots[k][:, q0:q0 + n, :].rearrange("p q v -> p (q v)"),
-            )
+        def s2_of(c):
+            return S2_EARLY if c <= 6 else S2_LATE
 
-        def store_all(k):
-            base = (k % 4) * CH * 800
-            nc.sync.dma_start(
-                out=of[k // 4, :, base:base + NQ * 20],
-                in_=ots[k][:].rearrange("p q v -> p (q v)"),
-            )
+        def copy_plane(c, s):
+            n = chunks[c][1]
+            ln = 4 * n
+            xr = xrs[c]
+            xs = (x2pool if s == 2 else xspool).tile([P, 5 * ln], BF16, align_bytes=64, name="xs")
+            xss[(c, s)] = xs
+            xv = xs[:].rearrange("p (j e) -> p j e", j=5)
+            if s == 2:
+                nc.scalar.copy(
+                    out=xs[:].bitcast(F32).rearrange("p (j e) -> p j e", j=5)[:, 0:s2_of(c), :],
+                    in_=xr[:].bitcast(F32)[:, 0:s2_of(c), 1:1 + ln // 2],
+                )
+            else:
+                nc.vector.tensor_copy(out=xv[:, 0:4, :], in_=xr[:, 0:4, s:s + ln])
+                nc.vector.tensor_copy(out=xv[:, 4, :], in_=xr[:, 4, s:s + ln])
 
-        def new_out(k):
-            ot = opool.tile([P, NQ, 20], F32, name="ot")
-            ots[k] = ot
+        def copy_plane2_rest(c):
+            ln = 4 * chunks[c][1]
+            xv = xss[(c, 2)][:].rearrange("p (j e) -> p j e", j=5)
+            for jb in range(s2_of(c), 5):
+                nc.vector.tensor_copy(out=xv[:, jb, :], in_=xrs[c][:, jb, 2:2 + ln])
 
-        def stage_groups(j0, j1):
-            for j in range(j0, j1):
-                for gi in range(2):
-                    transposes_pe(j, gi)
-                for gi in range(2):
-                    transposes_out(j, gi, gi)
+        def quantise(c, s):
+            n = chunks[c][1]
+            codes = cpool.tile([P, 5 * n], U32, align_bytes=64, name="codes")
+            scales = cpool.tile([P, 5 * n], U8, align_bytes=64, name="scales")
+            cds[(c, s)] = (codes, scales)
+            if s == 0:
+                for jb in range(5):
+                    nc.vector.quantize_mx(
+                        out=codes[:, jb * n:(jb + 1) * n].bitcast(FP8X4), scales=scales[:, jb * n:(jb + 1) * n],
+                        in_=xrs[c][:, jb, 0:4 * n],
+                    )
+                return
+            w = 0
+            while w < 5 * n:
+                step = [q for q in QW if q <= 5 * n - w][0]
+                nc.vector.quantize_mx(
+                    out=codes[:, w:w + step].bitcast(FP8X4), scales=scales[:, w:w + step],
+                    in_=xss[(c, s)][:, 4 * w:4 * (w + step)],
+                )
+                w += step
+
+        def passes(c, g):
+            w0, n = chunks[c]
+            for wi in range((n + WIN - 1) // WIN):
+                nn = min(WIN, n - wi * WIN)
+                acc = psum_m.tile([P, 4, WIN], F32, name="acc")
+                for v in range(4):
+                    s, jb = divmod(4 * g + v, 5)
+                    codes, scales = cds[(c, s)]
+                    o = jb * n + wi * WIN
+                    nc.tensor.matmul_mx(
+                        out=acc[:, v, 0:nn],
+                        lhsT=wcodes[:].bitcast(FP8X4), lhsT_scale=wscales[:],
+                        rhs=codes[:, o:o + nn].bitcast(FP8X4), rhs_scale=scales[:, o:o + nn],
+                        start=True, stop=True,
+                    )
+                base = ((w0 // WIN + wi) % RW) * WF
+                nc.scalar.activation(
+                    out=ring[:, base:base + 20 * nn].rearrange("p (q e) -> p q e", e=20)[:, :, 4 * g:4 * g + 4],
+                    in_=acc[:, :, 0:nn].rearrange("p v q -> p q v"),
+                    func=ACT.Identity, bias=bias_sb[:, 0:1], scale=1.0,
+                )
+
+        stored = {"c": 0}
+
+        def store(c):
+            w0, n = chunks[c]
+            done = 20 * (w0 + n)
+            c0 = stored["c"]
+            c1 = c0
+            while c1 < 64 and CPITCH * c1 + 800 <= done:
+                c1 += 1
+            stored["c"] = c1
+            a = c0
+            while a < c1:
+                lap = (CPITCH * a) // RINGF
+                pos = CPITCH * a - lap * RINGF
+                if (CPITCH * a + 799) // RINGF != lap:
+                    k = RINGF - pos
+                    nc.sync.dma_start(out=of[a // 32, :, (a % 32) * 800:(a % 32) * 800 + k], in_=ring[:, pos:RINGF])
+                    nc.sync.dma_start(out=of[a // 32, :, (a % 32) * 800 + k:(a % 32 + 1) * 800], in_=ring[:, 0:800 - k])
+                    a += 1
+                    continue
+                b = a + 1
+                while b < c1 and b // 32 == a // 32 and (CPITCH * b + 799) // RINGF == lap:
+                    b += 1
+                nc.sync.dma_start(
+                    out=of[a // 32, :, (a % 32) * 800:(a % 32 + b - a) * 800].rearrange("o (c e) -> o c e", e=800),
+                    in_=ring[:, pos:pos + CPITCH * (b - a)].rearrange("p (c e) -> p c e", e=CPITCH)[:, :, 0:800],
+                )
+                a = b
 
         diff = const.tile([P, P], I32)
         nc.gpsimd.iota(diff[:], pattern=[[1, 32], [1, 4]], base=0, channel_multiplier=-1)
@@ -264,8 +276,8 @@ def tile_conv2d_kernel(tc, x, weights, bias, out):
                 out=sel[:], in0=diff[:], scalar1=float(-ROW0[jb]), scalar2=None, op0=ALU.is_equal,
             )
             sels.append(sel)
-
-        for j in range(8):
+        xl = {"n": 10}
+        for j in range(xl["n"]):
             load_x(j)
         wg = const.tile([P, P, 4], BF16, align_bytes=64)
         nc.vector.tensor_copy(out=wg[:], in_=raw_w[:].rearrange("p i o -> p o i"))
@@ -275,99 +287,78 @@ def tile_conv2d_kernel(tc, x, weights, bias, out):
             out=wcodes[:].bitcast(FP8X4), scales=wscales[:],
             in_=wg[:].rearrange("p o i -> p (o i)"),
         )
-        stage_groups(0, 3)
-        for j in range(8, 12):
-            load_x(j)
 
-        xr_first = reppool.tile([P, 5, CLP], BF16, name="xr")
-        xrs[0] = xr_first
+        gmin = [4 * w0 // GF for (w0, n) in chunks]
+        gmax = [(4 * (w0 + n) + 3) // GF for (w0, n) in chunks]
+        st = {"pe": 0, "out": 0, "reloads": NPE}
 
-        def spread(jb):
-            src = xt[0] if jb < 3 else xt[1]
-            bank_a = psum_m.tile([P, 1024], BF16, name="acc")
-            bank_b = psum_m.tile([P, 1024], BF16, name="acc")
-            for (c0, n, bank, b0) in ((0, 512, bank_a, 0), (512, 512, bank_a, 512),
-                                      (1024, 256, bank_b, 0), (1280, 32, bank_b, 256)):
-                nc.tensor.matmul(
-                    out=bank[:, b0:b0 + n], lhsT=sels[jb][:], rhs=src[:, c0:c0 + n],
-                    start=True, stop=True,
-                )
-            evac(jb % 2 if jb < 3 else 1, xr_first[:, jb, 0:1024], bank_a[:])
-            evac(1 - jb % 2 if jb < 3 else 1, xr_first[:, jb, 1024:CL], bank_b[:, 0:CL - 1024])
+        def t_pe():
+            if st["pe"] < NG:
+                transposes_pe(st["pe"])
+                st["pe"] += 1
 
-        for jb in range(3):
-            spread(jb)
-        for j in range(3, 6):
-            for gi in range(2):
-                transposes_pe(j, gi)
-            for gi in range(2):
-                transposes_out(j, gi, 1)
-        park(1)
-        reload(1)
-        for j in range(12, NG):
-            load_x(j)
-        for jb in range(3, 5):
-            spread(jb)
-        for g in range(FIRST):
-            copies(0, g, 0)
-        pb = psum_t.tile([P, 4, P], BF16, name="pt")
-        nc.tensor.transpose(pb[:, 0, :], zb[:], ident[:])
-        bias_sb = const.tile([P, 1], F32)
-        nc.vector.tensor_copy(out=bias_sb[:], in_=pb[:, 0, 0:1])
-        for g in range(FIRST):
-            copies(0, g, 1)
+        def t_out(eng):
+            if st["out"] < st["pe"]:
+                j = st["out"]
+                transposes_out(j, eng)
+                st["out"] += 1
+                if (j % 2 == 1 or j == NG - 1) and j >= gmin[NPE]:
+                    park(j // 2)
 
-        units = [(k, g) for k in range(NK) for g in range(5)]
-        n_plain = 5 * (NK - 1)
-        st = {"groups": 6, "out": 6, "parks": 2, "reloads": 2, "copied": FIRST}
-
-        def try_reload():
+        def try_reload(i):
             r = st["reloads"]
-            if r < NK and st["parks"] > r and st["copied"] >= 5 * (r - XR_BUFS + 1):
+            if r < NC and gmax[r] < st["out"] and r - XR_BUFS <= i:
                 reload(r)
                 st["reloads"] += 1
 
-        def copy_ahead(upto):
-            while st["copied"] <= min(upto, len(units) - 1):
-                kk, gg = units[st["copied"]]
-                copies(kk, gg)
-                st["copied"] += 1
-                try_reload()
+        pb = psum_m.tile([P, 1024], BF16, name="acc")
+        nc.tensor.transpose(pb[:, 0:P], zb[:], ident[:])
+        bias_sb = const.tile([P, 1], F32)
+        nc.vector.tensor_copy(out=bias_sb[:], in_=pb[:, 0:1])
+        def t_take():
+            if st["out"] < NG:
+                t_out(TENG[st["out"]])
+                if xl["n"] < NG:
+                    load_x(xl["n"])
+                    xl["n"] += 1
 
-        copy_ahead(LOOK - 1)
-        for i in range(n_plain):
-            k, g = units[i]
-            copy_ahead(i + LOOK)
-            if g == 0:
-                new_out(k)
-            new_codes(k, g)
-            quantise(k, g, 0, 1024)
-            quantise(k, g, 1024, 1280)
-            if st["groups"] > st["out"]:
-                transposes_out(st["out"], 0, 1)
-                transposes_out(st["out"], 1, 1)
-                st["out"] += 1
-                while st["parks"] < NK and (CL * (st["parks"] + 1) - 1) // P < 4 * st["out"]:
-                    park(st["parks"])
-                    st["parks"] += 1
-                try_reload()
-            for wi in range(3):
-                passes(k, g, wi)
-            if g == 4:
-                store_all(k)
-            if st["groups"] < NG:
-                transposes_pe(st["groups"], 0)
-                transposes_pe(st["groups"], 1)
-                st["groups"] += 1
+        def t_step():
+            t_take()
+            t_pe()
 
-        k = NK - 1
-        copy_ahead(len(units) - 1)
-        new_out(k)
-        for g in range(5):
-            new_codes(k, g)
-        for wi, (w0, w1) in enumerate(((0, 128), (128, 256), (256, 320))):
-            for g in range(5):
-                for v in range(4):
-                    quantise(k, g, v * NQ + w0, v * NQ + w1)
-                passes(k, g, wi)
-            store(k, wi)
+        t_pe()
+        t_pe()
+        for j in range(6):
+            t_step()
+            for c in range(NPE):
+                if gmax[c] == j:
+                    spread(c, (0, 1, 0, 1, 0, 1) if c == 0 else (1, 1, 1, 1, 1, 1))
+                    if c == 0:
+                        copy_plane(0, 2)
+            try_reload(-1)
+
+        for i in range(NC):
+            copy_plane(i, 1)
+            copy_plane2_rest(i)
+            if i + 1 < NC:
+                copy_plane(i + 1, 2)
+            quantise(i, 0)
+            passes(i, 0)
+            if i > 0:
+                store(i - 1)
+            t_take()
+            quantise(i, 1)
+            copy_plane(i, 3)
+            passes(i, 1)
+            t_pe()
+            t_take()
+            quantise(i, 2)
+            passes(i, 2)
+            t_pe()
+            t_take()
+            quantise(i, 3)
+            try_reload(i)
+            passes(i, 3)
+            t_pe()
+            passes(i, 4)
+        store(NC - 1)

@@ -33,11 +33,11 @@ RINGF = RW * WF
 CPITCH = 5 * HW
 PKP = 5256
 PK0 = 25600 - 2 * PKP
-NPE = 2
+PESET = (0, 1, 4, 7, 11)
 XR_BUFS = 3
-S2_EARLY, S2_LATE = 4, 5
-TENG = (0, 1) + (1,) * 19
-TSTEPS = 3
+S2_PE, S2_DMA = 1, 4
+TENG = (0,) + (1,) * 10
+SP_ENG = (1, 1, 1, 1, 1)
 QW = (1024, 512, 256, 128, 64, 32)
 
 
@@ -106,42 +106,39 @@ def tile_conv2d_kernel(tc, x, weights, bias, out):
                     nc.tensor.transpose(pt[:, gi, u, :], xp[:, tl, gi * HI0:gi * HI0 + P], ident[:])
             pending[j] = pt
 
-        def transposes_out(j, eng):
-            if j % 2 == 0:
-                xb_new = xtpool.tile([P, 2, 2, GF], BF16, name="xb")
-                xbs[j // 2] = xb_new
-            xb = xbs[j // 2]
+        def transposes_out(j):
+            b, h = (j + 1) // 2, (j + 1) % 2
+            if b not in xbs:
+                xb_new = xtpool.tile([P, 2, 2 * GF], BF16, name="xb")
+                xbs[b] = xb_new
+            xb = xbs[b]
             pt = pending[j]
             if j < NG - 1:
-                evac(eng, xb[:, j % 2, :, :], pt[:].rearrange("p g u r -> p g (u r)"))
+                evac(TENG[b], xb[:, :, h * GF:(h + 1) * GF], pt[:].rearrange("p g u r -> p g (u r)"))
             else:
-                nc.gpsimd.memset(xb[:, 0, :, 192:272], 0.0)
-                evac(eng, xb[:, 0, :, 0:P], pt[:, :, 0, :])
-                evac(eng, xb[:, 0, :, P:192], pt[:, :, 1, 64:P])
+                nc.gpsimd.memset(xb[:, :, GF + 192:GF + 272], 0.0)
+                evac(TENG[b], xb[:, :, GF:GF + P], pt[:, :, 0, :])
+                evac(TENG[b], xb[:, :, GF + P:GF + 192], pt[:, :, 1, 64:P])
 
-        def group(j, gi, n):
-            return xbs[j // 2][:, j % 2, gi, 0:n]
+        def flat(f, gi, n):
+            j = f // GF
+            o = ((j + 1) % 2) * GF + f % GF
+            return xbs[(j + 1) // 2][:, gi, o:o + n]
 
-        def park(tb):
+        def park(b):
+            n = 2 * chunks[b][1]
             for gi in range(2):
-                col = PK0 + gi * PKP + GF * tb
-                if tb < NG // 2:
-                    nc.sync.dma_start(
-                        out=of[1, :, col:col + GF].rearrange("o (h c) -> o h c", h=2),
-                        in_=xbs[tb][:, :, gi, :].bitcast(F32),
-                    )
-                else:
-                    nc.sync.dma_start(out=of[1, :, col:col + 136], in_=xbs[tb][:, 0, gi, 0:272].bitcast(F32))
+                col = PK0 + gi * PKP + GF * b - GF // 2
+                nc.sync.dma_start(out=of[1, :, col:col + n], in_=xbs[b][:, gi, 0:2 * n].bitcast(F32))
 
         def new_xr(c):
             xr = xrpool.tile([P, 5, XRP], BF16, align_bytes=64, name="xr")
             xrs[c] = xr
-            return xr
 
         def reload(c):
             w0, n = chunks[c]
-            xr32 = new_xr(c)[:].bitcast(F32)
-            ln = 2 * n + 2
+            xr32 = xrs[c][:].bitcast(F32)
+            ln = 2 * n
             for gi, (j0, j1, r0) in enumerate(((0, 3, 0), (3, 5, 96 - HI0))):
                 col = PK0 + gi * PKP + 2 * w0
                 for dj in range(4):
@@ -150,28 +147,31 @@ def tile_conv2d_kernel(tc, x, weights, bias, out):
                         in_=of[1, r0 + dj:r0 + dj + 32 * (j1 - j0), col:col + ln].rearrange("(j m) c -> m j c", m=32),
                     )
 
-        def spread(c, engs):
+        def spread_jb(c, jb, eng):
             w0, n = chunks[c]
             f0, ln = 4 * w0, 4 * n
-            xr = new_xr(c)
+            gi = 0 if jb < 3 else 1
+            bank = psum_m.tile([P, 1024], BF16, name="acc")
+            for q in range(0, ln, GF):
+                k = min(GF, ln - q)
+                nc.tensor.matmul(
+                    out=bank[:, q:q + k], lhsT=sels[jb][:], rhs=flat(f0 + q, gi, k), start=True, stop=True,
+                )
+            evac(eng, xrs[c][:, jb, 0:ln], bank[:, 0:ln])
+
+        def overlap(c, eng):
+            w0, n = chunks[c]
+            f1 = 4 * (w0 + n)
             over = psum_m.tile([P, 1024], BF16, name="acc")
             for jb in range(5):
-                gi = 0 if jb < 3 else 1
-                bank = psum_m.tile([P, 1024], BF16, name="acc")
-                for q in range(ln // GF):
-                    nc.tensor.matmul(
-                        out=bank[:, GF * q:GF * (q + 1)], lhsT=sels[jb][:], rhs=group(f0 // GF + q, gi, GF),
-                        start=True, stop=True,
-                    )
                 nc.tensor.matmul(
-                    out=over[:, 4 * jb:4 * jb + 4], lhsT=sels[jb][:], rhs=group((f0 + ln) // GF, gi, 4),
+                    out=over[:, 4 * jb:4 * jb + 4], lhsT=sels[jb][:], rhs=flat(f1, 0 if jb < 3 else 1, 4),
                     start=True, stop=True,
                 )
-                evac(engs[jb], xr[:, jb, 0:ln], bank[:, 0:ln])
-            evac(engs[5], xr[:, :, ln:ln + 4], over[:, 0:20].rearrange("p (j e) -> p j e", e=4))
+            evac(eng, xrs[c][:, :, 4 * n:4 * n + 4], over[:, 0:20].rearrange("p (j e) -> p j e", e=4))
 
         def s2_of(c):
-            return S2_EARLY if c <= 6 else S2_LATE
+            return S2_PE if c + 1 in PESET and c + 1 < NC else S2_DMA
 
         def copy_plane(c, s):
             n = chunks[c][1]
@@ -181,10 +181,11 @@ def tile_conv2d_kernel(tc, x, weights, bias, out):
             xss[(c, s)] = xs
             xv = xs[:].rearrange("p (j e) -> p j e", j=5)
             if s == 2:
-                nc.scalar.copy(
-                    out=xs[:].bitcast(F32).rearrange("p (j e) -> p j e", j=5)[:, 0:s2_of(c), :],
-                    in_=xr[:].bitcast(F32)[:, 0:s2_of(c), 1:1 + ln // 2],
-                )
+                if s2_of(c) > 0:
+                    nc.scalar.copy(
+                        out=xs[:].bitcast(F32).rearrange("p (j e) -> p j e", j=5)[:, 0:s2_of(c), :],
+                        in_=xr[:].bitcast(F32)[:, 0:s2_of(c), 1:1 + ln // 2],
+                    )
             else:
                 nc.vector.tensor_copy(out=xv[:, 0:4, :], in_=xr[:, 0:4, s:s + ln])
                 nc.vector.tensor_copy(out=xv[:, 4, :], in_=xr[:, 4, s:s + ln])
@@ -192,8 +193,12 @@ def tile_conv2d_kernel(tc, x, weights, bias, out):
         def copy_plane2_rest(c):
             ln = 4 * chunks[c][1]
             xv = xss[(c, 2)][:].rearrange("p (j e) -> p j e", j=5)
-            for jb in range(s2_of(c), 5):
-                nc.vector.tensor_copy(out=xv[:, jb, :], in_=xrs[c][:, jb, 2:2 + ln])
+            k = s2_of(c)
+            if (5 - k) % 2 == 1:
+                nc.vector.tensor_copy(out=xv[:, k, :], in_=xrs[c][:, k, 2:2 + ln])
+                k += 1
+            if k < 5:
+                nc.vector.tensor_copy(out=xv[:, k:5, :], in_=xrs[c][:, k:5, 2:2 + ln])
 
         def quantise(c, s):
             n = chunks[c][1]
@@ -287,78 +292,91 @@ def tile_conv2d_kernel(tc, x, weights, bias, out):
             out=wcodes[:].bitcast(FP8X4), scales=wscales[:],
             in_=wg[:].rearrange("p o i -> p (o i)"),
         )
+        bias_sb = const.tile([P, 1], F32)
 
-        gmin = [4 * w0 // GF for (w0, n) in chunks]
-        gmax = [(4 * (w0 + n) + 3) // GF for (w0, n) in chunks]
-        st = {"pe": 0, "out": 0, "reloads": NPE}
+        st = {"pe": 0, "out": 0}
 
         def t_pe():
             if st["pe"] < NG:
                 transposes_pe(st["pe"])
                 st["pe"] += 1
 
-        def t_out(eng):
-            if st["out"] < st["pe"]:
-                j = st["out"]
-                transposes_out(j, eng)
-                st["out"] += 1
-                if (j % 2 == 1 or j == NG - 1) and j >= gmin[NPE]:
-                    park(j // 2)
-
-        def try_reload(i):
-            r = st["reloads"]
-            if r < NC and gmax[r] < st["out"] and r - XR_BUFS <= i:
-                reload(r)
-                st["reloads"] += 1
-
-        pb = psum_m.tile([P, 1024], BF16, name="acc")
-        nc.tensor.transpose(pb[:, 0:P], zb[:], ident[:])
-        bias_sb = const.tile([P, 1], F32)
-        nc.vector.tensor_copy(out=bias_sb[:], in_=pb[:, 0:1])
         def t_take():
             if st["out"] < NG:
-                t_out(TENG[st["out"]])
+                j = st["out"]
+                transposes_out(j)
+                st["out"] += 1
+                b = (j + 1) // 2
+                if b not in PESET and j == (4 * sum(chunks[b]) - 1) // GF:
+                    park(b)
                 if xl["n"] < NG:
                     load_x(xl["n"])
                     xl["n"] += 1
 
-        def t_step():
-            t_take()
-            t_pe()
-
         t_pe()
         t_pe()
-        for j in range(6):
-            t_step()
-            for c in range(NPE):
-                if gmax[c] == j:
-                    spread(c, (0, 1, 0, 1, 0, 1) if c == 0 else (1, 1, 1, 1, 1, 1))
-                    if c == 0:
-                        copy_plane(0, 2)
-            try_reload(-1)
+        t_take()
+        t_take()
+        new_xr(0)
+        for jb in range(5):
+            spread_jb(0, jb, jb % 2)
+        overlap(0, 1)
+        copy_plane(0, 2)
+        t_pe()
+        t_pe()
+        pb = psum_m.tile([P, 1024], BF16, name="acc")
+        nc.tensor.transpose(pb[:, 0:P], zb[:], ident[:])
+        nc.scalar.copy(out=bias_sb[:], in_=pb[:, 0:1])
+        t_take()
+        t_take()
+        new_xr(1)
+        for jb in range(5):
+            spread_jb(1, jb, 1)
+        overlap(1, 1)
+        t_pe()
+        t_pe()
+        t_take()
+        t_take()
+        t_pe()
+        t_pe()
 
         for i in range(NC):
+            r = i + 2 if i + 2 < NC else None
+            by_pe = r is not None and r in PESET
             copy_plane(i, 1)
             copy_plane2_rest(i)
             if i + 1 < NC:
                 copy_plane(i + 1, 2)
+            if r is not None:
+                new_xr(r)
+                if not by_pe:
+                    reload(r)
             quantise(i, 0)
             passes(i, 0)
             if i > 0:
                 store(i - 1)
             t_take()
+            if by_pe:
+                spread_jb(r, 0, SP_ENG[0])
             quantise(i, 1)
             copy_plane(i, 3)
             passes(i, 1)
             t_pe()
             t_take()
+            if by_pe:
+                spread_jb(r, 1, SP_ENG[1])
             quantise(i, 2)
             passes(i, 2)
             t_pe()
-            t_take()
+            if by_pe:
+                spread_jb(r, 2, SP_ENG[2])
             quantise(i, 3)
-            try_reload(i)
             passes(i, 3)
-            t_pe()
+            if by_pe:
+                spread_jb(r, 3, SP_ENG[3])
             passes(i, 4)
+            if by_pe:
+                spread_jb(r, 4, SP_ENG[4])
+            if r is not None:
+                overlap(r, 1)
         store(NC - 1)

@@ -33,11 +33,14 @@ RINGF = RW * WF
 CPITCH = 5 * HW
 PKP = 5256
 PK0 = 25600 - 2 * PKP
-PESET = (0, 1, 4, 7, 11)
+PESET = (0, 1, 5, 8, 11)
 XR_BUFS = 3
 S2_PE, S2_DMA = 1, 4
 TENG = (0,) + (1,) * 10
 SP_ENG = (1, 1, 1, 1, 1)
+PAIRS = ((3, 4), (6, 7), (9, 10))
+XR2_BUFS = 1
+XP_BUFS = 12
 QW = (1024, 512, 256, 128, 64, 32)
 
 
@@ -52,11 +55,13 @@ def tile_conv2d_kernel(tc, x, weights, bias, out):
 
     with ExitStack() as ctx:
         const = ctx.enter_context(tc.tile_pool(name="const", bufs=1))
+        xppool = ctx.enter_context(tc.tile_pool(name="xp", bufs=XP_BUFS))
         xtpool = ctx.enter_context(tc.tile_pool(name="xt", bufs=3))
         xrpool = ctx.enter_context(tc.tile_pool(name="rep", bufs=XR_BUFS))
+        xr2pool = ctx.enter_context(tc.tile_pool(name="rep2", bufs=XR2_BUFS))
         xspool = ctx.enter_context(tc.tile_pool(name="xs", bufs=2))
         x2pool = ctx.enter_context(tc.tile_pool(name="xs2", bufs=2))
-        cpool = ctx.enter_context(tc.tile_pool(name="cp", bufs=7))
+        cpool = ctx.enter_context(tc.tile_pool(name="cp", bufs=5))
         psum_t = ctx.enter_context(tc.psum_pool(name="pst", bufs=2))
         psum_m = ctx.enter_context(tc.psum_pool(name="psm", bufs=6))
         ctx.enter_context(tc.manual_schedule())
@@ -77,7 +82,7 @@ def tile_conv2d_kernel(tc, x, weights, bias, out):
         def load_x(j):
             spans = [(4 * j, 4 * j + 4)] if j < NG - 1 else [(80, 81), (81, 82)]
             for (t0, t1) in spans:
-                xp = const.tile([P, t1 - t0, XPITCH], BF16, name="xp%d" % t0)
+                xp = xppool.tile([P, t1 - t0, XPITCH], BF16, name="xp")
                 r0 = min(P * t0, ROWS - P)
                 nc.sync.dma_start(
                     out=xp[:, :, 0:HW],
@@ -93,6 +98,10 @@ def tile_conv2d_kernel(tc, x, weights, bias, out):
                 nc.scalar.copy(out=dst, in_=src)
 
         pending = {}
+        mate = dict(PAIRS)
+        seconds = [b for (a, b) in PAIRS]
+        xb2 = {}
+        xr2 = {}
         xbs = {}
         xrs = {}
         xss = {}
@@ -109,14 +118,23 @@ def tile_conv2d_kernel(tc, x, weights, bias, out):
         def transposes_out(j):
             b, h = (j + 1) // 2, (j + 1) % 2
             if b not in xbs:
-                xb_new = xtpool.tile([P, 2, 2 * GF], BF16, name="xb")
-                xbs[b] = xb_new
+                if b in mate:
+                    xb_two = xtpool.tile([P, 2, 4 * GF], BF16, name="xb")
+                    xbs[b] = xb_two[:, :, 0:2 * GF]
+                    xbs[mate[b]] = xb_two[:, :, 2 * GF:4 * GF]
+                    xb2[b] = xb_two
+                    if mate[b] == NG // 2:
+                        nc.gpsimd.memset(xb_two[:, :, 3 * GF + 192:3 * GF + 272], 0.0)
+                else:
+                    xb_new = xtpool.tile([P, 2, 2 * GF], BF16, name="xb")
+                    xbs[b] = xb_new
+                    if b == NG // 2:
+                        nc.gpsimd.memset(xb_new[:, :, GF + 192:GF + 272], 0.0)
             xb = xbs[b]
             pt = pending[j]
             if j < NG - 1:
                 evac(TENG[b], xb[:, :, h * GF:(h + 1) * GF], pt[:].rearrange("p g u r -> p g (u r)"))
             else:
-                nc.gpsimd.memset(xb[:, :, GF + 192:GF + 272], 0.0)
                 evac(TENG[b], xb[:, :, GF:GF + P], pt[:, :, 0, :])
                 evac(TENG[b], xb[:, :, GF + P:GF + 192], pt[:, :, 1, 64:P])
 
@@ -126,19 +144,26 @@ def tile_conv2d_kernel(tc, x, weights, bias, out):
             return xbs[(j + 1) // 2][:, gi, o:o + n]
 
         def park(b):
-            n = 2 * chunks[b][1]
+            n = 2 * (chunks[b][1] + (chunks[mate[b]][1] if b in mate else 0))
+            src = xb2[b] if b in mate else xbs[b]
             for gi in range(2):
                 col = PK0 + gi * PKP + GF * b - GF // 2
-                nc.sync.dma_start(out=of[1, :, col:col + n], in_=xbs[b][:, gi, 0:2 * n].bitcast(F32))
+                nc.sync.dma_start(out=of[1, :, col:col + n], in_=src[:, gi, 0:2 * n].bitcast(F32))
 
         def new_xr(c):
-            xr = xrpool.tile([P, 5, XRP], BF16, align_bytes=64, name="xr")
-            xrs[c] = xr
+            if c in mate:
+                xr_two = xr2pool.tile([P, 5, XRP + 4 * NMAX], BF16, align_bytes=64, name="xr2")
+                xrs[c] = xr_two[:, :, 0:XRP]
+                xrs[mate[c]] = xr_two[:, :, 4 * NMAX:4 * NMAX + XRP]
+                xr2[c] = xr_two
+            else:
+                xr = xrpool.tile([P, 5, XRP], BF16, align_bytes=64, name="xr")
+                xrs[c] = xr
 
         def reload(c):
             w0, n = chunks[c]
-            xr32 = xrs[c][:].bitcast(F32)
-            ln = 2 * n
+            xr32 = (xr2[c] if c in mate else xrs[c])[:].bitcast(F32)
+            ln = 2 * (n + (chunks[mate[c]][1] if c in mate else 0))
             for gi, (j0, j1, r0) in enumerate(((0, 3, 0), (3, 5, 96 - HI0))):
                 col = PK0 + gi * PKP + 2 * w0
                 for dj in range(4):
@@ -307,8 +332,8 @@ def tile_conv2d_kernel(tc, x, weights, bias, out):
                 transposes_out(j)
                 st["out"] += 1
                 b = (j + 1) // 2
-                if b not in PESET and j == (4 * sum(chunks[b]) - 1) // GF:
-                    park(b)
+                if b not in PESET and b not in mate and j == (4 * sum(chunks[b]) - 1) // GF:
+                    park(b - 1 if b in seconds else b)
                 if xl["n"] < NG:
                     load_x(xl["n"])
                     xl["n"] += 1
@@ -339,17 +364,23 @@ def tile_conv2d_kernel(tc, x, weights, bias, out):
         t_take()
         t_pe()
         t_pe()
+        t_take()
+        t_take()
+        t_pe()
+        t_pe()
 
         for i in range(NC):
             r = i + 2 if i + 2 < NC else None
             by_pe = r is not None and r in PESET
+            late2 = XR2_BUFS == 1 and i + 1 in mate
             copy_plane(i, 1)
             copy_plane2_rest(i)
-            if i + 1 < NC:
+            if i + 1 < NC and not late2:
                 copy_plane(i + 1, 2)
-            if r is not None:
+            if r is not None and r not in seconds and not (r in mate and XR2_BUFS == 1):
                 new_xr(r)
                 if not by_pe:
+                    overlap(mate.get(r, r), 1)
                     reload(r)
             quantise(i, 0)
             passes(i, 0)
@@ -360,6 +391,10 @@ def tile_conv2d_kernel(tc, x, weights, bias, out):
                 spread_jb(r, 0, SP_ENG[0])
             quantise(i, 1)
             copy_plane(i, 3)
+            if r is not None and r in mate and XR2_BUFS == 1:
+                new_xr(r)
+                overlap(mate[r], 1)
+                reload(r)
             passes(i, 1)
             t_pe()
             t_take()
@@ -371,12 +406,14 @@ def tile_conv2d_kernel(tc, x, weights, bias, out):
             if by_pe:
                 spread_jb(r, 2, SP_ENG[2])
             quantise(i, 3)
+            if late2:
+                copy_plane(i + 1, 2)
             passes(i, 3)
             if by_pe:
                 spread_jb(r, 3, SP_ENG[3])
             passes(i, 4)
             if by_pe:
                 spread_jb(r, 4, SP_ENG[4])
-            if r is not None:
+            if by_pe:
                 overlap(r, 1)
         store(NC - 1)

@@ -198,6 +198,9 @@ def tile_conv2d_kernel(tc, x, weights, bias, out):
         def s2_of(c):
             return S2_PE if c + 1 in PESET and c + 1 < NC else S2_DMA
 
+        def by_dma(c):
+            return c > 0 and c + 1 in PESET
+
         def copy_plane(c, s):
             n = chunks[c][1]
             ln = 4 * n
@@ -205,7 +208,11 @@ def tile_conv2d_kernel(tc, x, weights, bias, out):
             xs = (x2pool if s == 2 else xspool).tile([P, 5 * ln], BF16, align_bytes=64, name="xs")
             xss[(c, s)] = xs
             xv = xs[:].rearrange("p (j e) -> p j e", j=5)
-            if s == 2:
+            if s == 2 and by_dma(c):
+                nc.sync.dma_start(
+                    out=xs[:].bitcast(F32).rearrange("p (j e) -> p j e", j=5), in_=xr[:].bitcast(F32)[:, :, 1:1 + ln // 2],
+                )
+            elif s == 2:
                 if s2_of(c) > 0:
                     nc.scalar.copy(
                         out=xs[:].bitcast(F32).rearrange("p (j e) -> p j e", j=5)[:, 0:s2_of(c), :],
@@ -216,6 +223,8 @@ def tile_conv2d_kernel(tc, x, weights, bias, out):
                 nc.vector.tensor_copy(out=xv[:, 4, :], in_=xr[:, 4, s:s + ln])
 
         def copy_plane2_rest(c):
+            if by_dma(c):
+                return
             ln = 4 * chunks[c][1]
             xv = xss[(c, 2)][:].rearrange("p (j e) -> p j e", j=5)
             k = s2_of(c)

@@ -64,7 +64,6 @@ def tile_conv2d_kernel(tc, x, weights, bias, out):
         cpool = ctx.enter_context(tc.tile_pool(name="cp", bufs=5))
         psum_t = ctx.enter_context(tc.psum_pool(name="pst", bufs=2))
         psum_m = ctx.enter_context(tc.psum_pool(name="psm", bufs=6))
-        ctx.enter_context(tc.manual_schedule())
 
         ident = const.tile([P, P], BF16)
         make_identity(nc, ident[:])

@@ -40,6 +40,7 @@ TENG = (0,) + (1,) * 10
 SP_ENG = (1, 1, 1, 1, 1)
 PAIRS = ((3, 4), (6, 7), (9, 10))
 XR2_BUFS = 1
+S2_FROM = 3
 XP_BUFS = 12
 QW = (1024, 512, 256, 128, 64, 32)
 
@@ -65,15 +66,13 @@ def tile_conv2d_kernel(tc, x, weights, bias, out):
         psum_t = ctx.enter_context(tc.psum_pool(name="pst", bufs=2))
         psum_m = ctx.enter_context(tc.psum_pool(name="psm", bufs=6))
 
+        ctx.enter_context(tc.manual_schedule(engines={mybir.EngineType.DVE}))
         ident = const.tile([P, P], BF16)
         make_identity(nc, ident[:])
         zb = const.tile([P, P], BF16)
         nc.vector.memset(zb[:], 0.0)
-        nc.scalar.dma_start(out=zb[0:1, :], in_=bias.rearrange("(o c) -> o c", o=1))
         raw_w = const.tile([P, 4, P], BF16)
-        w_view = weights.rearrange("(m i j) o -> j m i o", i=4, j=4)
-        for dj in range(4):
-            nc.scalar.dma_start(out=raw_w[dj:P:4, :, :], in_=w_view[dj])
+        bias_sb = const.tile([P, 1], F32)
         ring = const.tile([P, RINGF + 16], F32)
 
         x_of_tile = {}
@@ -195,6 +194,8 @@ def tile_conv2d_kernel(tc, x, weights, bias, out):
             evac(eng, xrs[c][:, :, 4 * n:4 * n + 4], over[:, 0:20].rearrange("p (j e) -> p j e", e=4))
 
         def s2_of(c):
+            if c < S2_FROM:
+                return 0
             return S2_PE if c + 1 in PESET and c + 1 < NC else S2_DMA
 
         def by_dma(c):
@@ -315,17 +316,15 @@ def tile_conv2d_kernel(tc, x, weights, bias, out):
             )
             sels.append(sel)
         xl = {"n": 10}
-        for j in range(xl["n"]):
+        for j in range(2):
             load_x(j)
-        wg = const.tile([P, P, 4], BF16, align_bytes=64)
-        nc.vector.tensor_copy(out=wg[:], in_=raw_w[:].rearrange("p i o -> p o i"))
-        wcodes = const.tile([P, P], U32, align_bytes=64)
-        wscales = const.tile([P, P], U8, align_bytes=64)
-        nc.vector.quantize_mx(
-            out=wcodes[:].bitcast(FP8X4), scales=wscales[:],
-            in_=wg[:].rearrange("p o i -> p (o i)"),
-        )
-        bias_sb = const.tile([P, 1], F32)
+        nc.scalar.activation(out=bias_sb[:], in_=zb[:, 0:1], func=ACT.Identity, bias=0.0, scale=1.0)
+        w_view = weights.rearrange("(m i j) o -> j m i o", i=4, j=4)
+        for dj in range(4):
+            nc.scalar.dma_start(out=raw_w[dj:P:4, :, :], in_=w_view[dj])
+        nc.scalar.dma_start(out=zb[0:1, :], in_=bias.rearrange("(o c) -> o c", o=1))
+        for j in range(2, xl["n"]):
+            load_x(j)
 
         st = {"pe": 0, "out": 0}
 
@@ -354,6 +353,14 @@ def tile_conv2d_kernel(tc, x, weights, bias, out):
         for jb in range(5):
             spread_jb(0, jb, jb % 2)
         overlap(0, 1)
+        wg = const.tile([P, P, 4], BF16, align_bytes=64)
+        nc.vector.tensor_copy(out=wg[:], in_=raw_w[:].rearrange("p i o -> p o i"))
+        wcodes = const.tile([P, P], U32, align_bytes=64)
+        wscales = const.tile([P, P], U8, align_bytes=64)
+        nc.vector.quantize_mx(
+            out=wcodes[:].bitcast(FP8X4), scales=wscales[:],
+            in_=wg[:].rearrange("p o i -> p (o i)"),
+        )
         copy_plane(0, 2)
         t_pe()
         t_pe()

@@ -40,7 +40,7 @@ TENG = (0,) + (1,) * 10
 SP_ENG = (1, 1, 1, 1, 1)
 PAIRS = ((3, 4), (6, 7), (9, 10))
 XR2_BUFS = 1
-S2_FROM = 3
+S2_FROM = 4
 XP_BUFS = 12
 QW = (1024, 512, 256, 128, 64, 32)
 
@@ -66,7 +66,7 @@ def tile_conv2d_kernel(tc, x, weights, bias, out):
         psum_t = ctx.enter_context(tc.psum_pool(name="pst", bufs=2))
         psum_m = ctx.enter_context(tc.psum_pool(name="psm", bufs=6))
 
-        ctx.enter_context(tc.manual_schedule(engines={mybir.EngineType.DVE}))
+        ctx.enter_context(tc.manual_schedule(engines={mybir.EngineType.DVE, mybir.EngineType.PE}))
         ident = const.tile([P, P], BF16)
         make_identity(nc, ident[:])
         zb = const.tile([P, P], BF16)
@@ -219,8 +219,10 @@ def tile_conv2d_kernel(tc, x, weights, bias, out):
                         in_=xr[:].bitcast(F32)[:, 0:s2_of(c), 1:1 + ln // 2],
                     )
             else:
-                nc.vector.tensor_copy(out=xv[:, 0:4, :], in_=xr[:, 0:4, s:s + ln])
-                nc.vector.tensor_copy(out=xv[:, 4, :], in_=xr[:, 4, s:s + ln])
+                nc.vector.tensor_copy(
+                    out=xv.rearrange("p j (h e) -> p h j e", h=2),
+                    in_=xr[:, :, s:s + ln].rearrange("p j (h e) -> p h j e", h=2),
+                )
 
         def copy_plane2_rest(c):
             if by_dma(c):
@@ -228,11 +230,11 @@ def tile_conv2d_kernel(tc, x, weights, bias, out):
             ln = 4 * chunks[c][1]
             xv = xss[(c, 2)][:].rearrange("p (j e) -> p j e", j=5)
             k = s2_of(c)
-            if (5 - k) % 2 == 1:
-                nc.vector.tensor_copy(out=xv[:, k, :], in_=xrs[c][:, k, 2:2 + ln])
-                k += 1
             if k < 5:
-                nc.vector.tensor_copy(out=xv[:, k:5, :], in_=xrs[c][:, k:5, 2:2 + ln])
+                nc.vector.tensor_copy(
+                    out=xv[:, k:5, :].rearrange("p j (h e) -> p h j e", h=2),
+                    in_=xrs[c][:, k:5, 2:2 + ln].rearrange("p j (h e) -> p h j e", h=2),
+                )
 
         def quantise(c, s):
             n = chunks[c][1]
@@ -377,53 +379,67 @@ def tile_conv2d_kernel(tc, x, weights, bias, out):
         t_pe()
         t_take()
         t_take()
-        t_pe()
-        t_pe()
-        t_take()
-        t_take()
-        t_pe()
-        t_pe()
+
+        START = (("t", "te", "te", "t", ""), ("", "t", "te", "e", ""), ("tt", "", "e", "e", "tt"))
+        LATER = ("e", "e", "", "", "tt")
 
         for i in range(NC):
             r = i + 2 if i + 2 < NC else None
             by_pe = r is not None and r in PESET
-            late2 = XR2_BUFS == 1 and i + 1 in mate
+            late2 = i + 1 in mate
+            plan = START[i] if i < len(START) else LATER
+
+            def more(g):
+                for what in plan[g]:
+                    if what == "t":
+                        t_pe()
+                    else:
+                        t_take()
+
+            def fetch_pair():
+                new_xr(r)
+                overlap(mate[r], 1)
+                reload(r)
+
             copy_plane(i, 1)
             copy_plane2_rest(i)
             if i + 1 < NC and not late2:
                 copy_plane(i + 1, 2)
-            if r is not None and r not in seconds and not (r in mate and XR2_BUFS == 1):
+            if by_pe:
                 new_xr(r)
-                if not by_pe:
-                    overlap(mate.get(r, r), 1)
-                    reload(r)
+            elif r == 2:
+                new_xr(r)
+                overlap(r, 1)
+                reload(r)
             quantise(i, 0)
+            if i == 1:
+                t_take()
+                t_take()
+                fetch_pair()
             passes(i, 0)
             if i > 0:
                 store(i - 1)
-            t_take()
+            more(0)
             if by_pe:
                 spread_jb(r, 0, SP_ENG[0])
             quantise(i, 1)
             copy_plane(i, 3)
-            if r is not None and r in mate and XR2_BUFS == 1:
-                new_xr(r)
-                overlap(mate[r], 1)
-                reload(r)
+            if i > 1 and r in mate:
+                fetch_pair()
             passes(i, 1)
-            t_pe()
-            t_take()
+            more(1)
             if by_pe:
                 spread_jb(r, 1, SP_ENG[1])
             quantise(i, 2)
             passes(i, 2)
-            t_pe()
+            more(2)
             if by_pe:
                 spread_jb(r, 2, SP_ENG[2])
             quantise(i, 3)
             if late2:
                 copy_plane(i + 1, 2)
             passes(i, 3)
+            more(3)
             if by_pe:
                 spread_jb(r, 3, SP_ENG[3])
             passes(i, 4)
@@ -431,4 +447,5 @@ def tile_conv2d_kernel(tc, x, weights, bias, out):
                 spread_jb(r, 4, SP_ENG[4])
             if by_pe:
                 overlap(r, 1)
+            more(4)
         store(NC - 1)

@@ -35,12 +35,12 @@ PKP = 5256
 PK0 = 25600 - 2 * PKP
 PESET = (0, 1, 5, 8, 11)
 XR_BUFS = 3
-S2_PE, S2_DMA = 1, 4
+S2_PE, S2_DMA = 1, 5
 TENG = (0,) + (1,) * 10
 SP_ENG = (1, 1, 1, 1, 1)
 PAIRS = ((3, 4), (6, 7), (9, 10))
 XR2_BUFS = 1
-S2_FROM = 4
+S2_FROM = 2
 XP_BUFS = 12
 QW = (1024, 512, 256, 128, 64, 32)
 

@@ -41,7 +41,7 @@ SP_ENG = (1, 1, 1, 1, 1)
 PAIRS = ((3, 4), (6, 7), (9, 10))
 XR2_BUFS = 1
 S2_FROM = 2
-XP_BUFS = 12
+XP_BUFS = 18
 QW = (1024, 512, 256, 128, 64, 32)
 
 
@@ -317,7 +317,7 @@ def tile_conv2d_kernel(tc, x, weights, bias, out):
                 out=sel[:], in0=diff[:], scalar1=float(-ROW0[jb]), scalar2=None, op0=ALU.is_equal,
             )
             sels.append(sel)
-        xl = {"n": 10}
+        xl = {"n": 16}
         for j in range(2):
             load_x(j)
         nc.scalar.activation(out=bias_sb[:], in_=zb[:, 0:1], func=ACT.Identity, bias=0.0, scale=1.0)

from contextlib import ExitStack

import concourse.mybir as mybir
from concourse.masks import make_identity

BF16 = mybir.dt.bfloat16
F32 = mybir.dt.float32
U32 = mybir.dt.uint32
U8 = mybir.dt.uint8
I32 = mybir.dt.int32
FP8X4 = mybir.dt.float8_e4m3fn_x4
ACT = mybir.ActivationFunctionType
ALU = mybir.AluOpType

FLOPS = 2 * 51200 * 512 * 128

P = 128
HW = 163
ROWS = 64 * HW
NT = 82
NG = 21
GF = 512
HI0 = 35
XPITCH = 176
ROW0 = (0, 32, 64, 96 - HI0, 128 - HI0)
CHUNK_WORDS = (128,) + (256,) * 9 + (128, 64)
NMAX = 256
XRP = 4 * NMAX + 32
WIN = 128
RW = 6
WF = 20 * WIN
RINGF = RW * WF
CPITCH = 5 * HW
PKP = 5256
PK0 = 25600 - 2 * PKP
PESET = (0, 1, 5, 8, 11)
XR_BUFS = 3
S2_PE, S2_DMA = 1, 5
TENG = (0,) + (1,) * 10
SP_ENG = (1, 1, 1, 1, 1)
PAIRS = ((3, 4), (6, 7), (9, 10))
XR2_BUFS = 1
S2_FROM = 2
XP_BUFS = 18
QW = (1024, 512, 256, 128, 64, 32)


def tile_conv2d_kernel(tc, x, weights, bias, out):
    nc = tc.nc
    x_rows = x.rearrange("b c h w -> (b c h) w")
    of = out.rearrange("b o u v -> b o (u v)")
    chunks = []
    for n in CHUNK_WORDS:
        chunks.append((sum(c[1] for c in chunks), n))
    NC = len(chunks)

    with ExitStack() as ctx:
        const = ctx.enter_context(tc.tile_pool(name="const", bufs=1))
        xppool = ctx.enter_context(tc.tile_pool(name="xp", bufs=XP_BUFS))
        xtpool = ctx.enter_context(tc.tile_pool(name="xt", bufs=3))
        xrpool = ctx.enter_context(tc.tile_pool(name="rep", bufs=XR_BUFS))
        xr2pool = ctx.enter_context(tc.tile_pool(name="rep2", bufs=XR2_BUFS))
        xspool = ctx.enter_context(tc.tile_pool(name="xs", bufs=2))
        x2pool = ctx.enter_context(tc.tile_pool(name="xs2", bufs=2))
        cpool = ctx.enter_context(tc.tile_pool(name="cp", bufs=5))
        psum_t = ctx.enter_context(tc.psum_pool(name="pst", bufs=2))
        psum_m = ctx.enter_context(tc.psum_pool(name="psm", bufs=6))

        ctx.enter_context(tc.manual_schedule(engines={mybir.EngineType.DVE, mybir.EngineType.PE}))
        ident = const.tile([P, P], BF16)
        make_identity(nc, ident[:])
        zb = const.tile([P, P], BF16)
        nc.vector.memset(zb[:], 0.0)
        raw_w = const.tile([P, 4, P], BF16)
        bias_sb = const.tile([P, 1], F32)
        ring = const.tile([P, RINGF + 16], F32)

        x_of_tile = {}

        def load_x(j):
            spans = [(4 * j, 4 * j + 4)] if j < NG - 1 else [(80, 81), (81, 82)]
            for (t0, t1) in spans:
                xp = xppool.tile([P, t1 - t0, XPITCH], BF16, name="xp")
                r0 = min(P * t0, ROWS - P)
                nc.sync.dma_start(
                    out=xp[:, :, 0:HW],
                    in_=x_rows[r0:r0 + P * (t1 - t0), :].rearrange("(t p) w -> p t w", p=P),
                )
                for t in range(t0, t1):
                    x_of_tile[t] = (xp, t - t0)

        def evac(eng, dst, src):
            if eng == 0:
                nc.vector.tensor_copy(out=dst, in_=src)
            else:
                nc.scalar.copy(out=dst, in_=src)

        pending = {}
        mate = dict(PAIRS)
        seconds = [b for (a, b) in PAIRS]
        xb2 = {}
        xr2 = {}
        xbs = {}
        xrs = {}
        xss = {}
        cds = {}

        def transposes_pe(j):
            pt = psum_t.tile([P, 2, 4, P], BF16, name="pt")
            for gi in range(2):
                for u in range(min(4, NT - 4 * j)):
                    xp, tl = x_of_tile[4 * j + u]
                    nc.tensor.transpose(pt[:, gi, u, :], xp[:, tl, gi * HI0:gi * HI0 + P], ident[:])
            pending[j] = pt

        def transposes_out(j):
            b, h = (j + 1) // 2, (j + 1) % 2
            if b not in xbs:
                if b in mate:
                    xb_two = xtpool.tile([P, 2, 4 * GF], BF16, name="xb")
                    xbs[b] = xb_two[:, :, 0:2 * GF]
                    xbs[mate[b]] = xb_two[:, :, 2 * GF:4 * GF]
                    xb2[b] = xb_two
                    if mate[b] == NG // 2:
                        nc.gpsimd.memset(xb_two[:, :, 3 * GF + 192:3 * GF + 272], 0.0)
                else:
                    xb_new = xtpool.tile([P, 2, 2 * GF], BF16, name="xb")
                    xbs[b] = xb_new
                    if b == NG // 2:
                        nc.gpsimd.memset(xb_new[:, :, GF + 192:GF + 272], 0.0)
            xb = xbs[b]
            pt = pending[j]
            if j < NG - 1:
                evac(TENG[b], xb[:, :, h * GF:(h + 1) * GF], pt[:].rearrange("p g u r -> p g (u r)"))
            else:
                evac(TENG[b], xb[:, :, GF:GF + P], pt[:, :, 0, :])
                evac(TENG[b], xb[:, :, GF + P:GF + 192], pt[:, :, 1, 64:P])

        def flat(f, gi, n):
            j = f // GF
            o = ((j + 1) % 2) * GF + f % GF
            return xbs[(j + 1) // 2][:, gi, o:o + n]

        def park(b):
            n = 2 * (chunks[b][1] + (chunks[mate[b]][1] if b in mate else 0))
            src = xb2[b] if b in mate else xbs[b]
            for gi in range(2):
                col = PK0 + gi * PKP + GF * b - GF // 2
                nc.sync.dma_start(out=of[1, :, col:col + n], in_=src[:, gi, 0:2 * n].bitcast(F32))

        def new_xr(c):
            if c in mate:
                xr_two = xr2pool.tile([P, 5, XRP + 4 * NMAX], BF16, align_bytes=64, name="xr2")
                xrs[c] = xr_two[:, :, 0:XRP]
                xrs[mate[c]] = xr_two[:, :, 4 * NMAX:4 * NMAX + XRP]
                xr2[c] = xr_two
            else:
                xr = xrpool.tile([P, 5, XRP], BF16, align_bytes=64, name="xr")
                xrs[c] = xr

        def reload(c):
            w0, n = chunks[c]
            xr32 = (xr2[c] if c in mate else xrs[c])[:].bitcast(F32)
            ln = 2 * (n + (chunks[mate[c]][1] if c in mate else 0))
            for gi, (j0, j1, r0) in enumerate(((0, 3, 0), (3, 5, 96 - HI0))):
                col = PK0 + gi * PKP + 2 * w0
                for dj in range(4):
                    nc.sync.dma_start(
                        out=xr32[dj:P:4, j0:j1, 0:ln],
                        in_=of[1, r0 + dj:r0 + dj + 32 * (j1 - j0), col:col + ln].rearrange("(j m) c -> m j c", m=32),
                    )

        def spread_jb(c, jb, eng):
            w0, n = chunks[c]
            f0, ln = 4 * w0, 4 * n
            gi = 0 if jb < 3 else 1
            bank = psum_m.tile([P, 1024], BF16, name="acc")
            for q in range(0, ln, GF):
                k = min(GF, ln - q)
                nc.tensor.matmul(
                    out=bank[:, q:q + k], lhsT=sels[jb][:], rhs=flat(f0 + q, gi, k), start=True, stop=True,
                )
            evac(eng, xrs[c][:, jb, 0:ln], bank[:, 0:ln])

        def overlap(c, eng):
            w0, n = chunks[c]
            f1 = 4 * (w0 + n)
            over = psum_m.tile([P, 1024], BF16, name="acc")
            for jb in range(5):
                nc.tensor.matmul(
                    out=over[:, 4 * jb:4 * jb + 4], lhsT=sels[jb][:], rhs=flat(f1, 0 if jb < 3 else 1, 4),
                    start=True, stop=True,
                )
            evac(eng, xrs[c][:, :, 4 * n:4 * n + 4], over[:, 0:20].rearrange("p (j e) -> p j e", e=4))

        def s2_of(c):
            if c < S2_FROM:
                return 0
            return S2_PE if c + 1 in PESET and c + 1 < NC else S2_DMA

        def by_dma(c):
            return c > 0 and c + 1 in PESET

        def copy_plane(c, s):
            n = chunks[c][1]
            ln = 4 * n
            xr = xrs[c]
            xs = (x2pool if s == 2 else xspool).tile([P, 5 * ln], BF16, align_bytes=64, name="xs")
            xss[(c, s)] = xs
            xv = xs[:].rearrange("p (j e) -> p j e", j=5)
            if s == 2 and by_dma(c):
                nc.sync.dma_start(
                    out=xs[:].bitcast(F32).rearrange("p (j e) -> p j e", j=5), in_=xr[:].bitcast(F32)[:, :, 1:1 + ln // 2],
                )
            elif s == 2:
                if s2_of(c) > 0:
                    nc.scalar.copy(
                        out=xs[:].bitcast(F32).rearrange("p (j e) -> p j e", j=5)[:, 0:s2_of(c), :],
                        in_=xr[:].bitcast(F32)[:, 0:s2_of(c), 1:1 + ln // 2],
                    )
            else:
                nc.vector.tensor_copy(
                    out=xv.rearrange("p j (h e) -> p h j e", h=2),
                    in_=xr[:, :, s:s + ln].rearrange("p j (h e) -> p h j e", h=2),
                )

        def copy_plane2_rest(c):
            if by_dma(c):
                return
            ln = 4 * chunks[c][1]
            xv = xss[(c, 2)][:].rearrange("p (j e) -> p j e", j=5)
            k = s2_of(c)
            if k < 5:
                nc.vector.tensor_copy(
                    out=xv[:, k:5, :].rearrange("p j (h e) -> p h j e", h=2),
                    in_=xrs[c][:, k:5, 2:2 + ln].rearrange("p j (h e) -> p h j e", h=2),
                )

        def quantise(c, s):
            n = chunks[c][1]
            codes = cpool.tile([P, 5 * n], U32, align_bytes=64, name="codes")
            scales = cpool.tile([P, 5 * n], U8, align_bytes=64, name="scales")
            cds[(c, s)] = (codes, scales)
            if s == 0:
                for jb in range(5):
                    nc.vector.quantize_mx(
                        out=codes[:, jb * n:(jb + 1) * n].bitcast(FP8X4), scales=scales[:, jb * n:(jb + 1) * n],
                        in_=xrs[c][:, jb, 0:4 * n],
                    )
                return
            w = 0
            while w < 5 * n:
                step = [q for q in QW if q <= 5 * n - w][0]
                nc.vector.quantize_mx(
                    out=codes[:, w:w + step].bitcast(FP8X4), scales=scales[:, w:w + step],
                    in_=xss[(c, s)][:, 4 * w:4 * (w + step)],
                )
                w += step

        def passes(c, g):
            w0, n = chunks[c]
            for wi in range((n + WIN - 1) // WIN):
                nn = min(WIN, n - wi * WIN)
                acc = psum_m.tile([P, 4, WIN], F32, name="acc")
                for v in range(4):
                    s, jb = divmod(4 * g + v, 5)
                    codes, scales = cds[(c, s)]
                    o = jb * n + wi * WIN
                    nc.tensor.matmul_mx(
                        out=acc[:, v, 0:nn],
                        lhsT=wcodes[:].bitcast(FP8X4), lhsT_scale=wscales[:],
                        rhs=codes[:, o:o + nn].bitcast(FP8X4), rhs_scale=scales[:, o:o + nn],
                        start=True, stop=True,
                    )
                base = ((w0 // WIN + wi) % RW) * WF
                nc.scalar.activation(
                    out=ring[:, base:base + 20 * nn].rearrange("p (q e) -> p q e", e=20)[:, :, 4 * g:4 * g + 4],
                    in_=acc[:, :, 0:nn].rearrange("p v q -> p q v"),
                    func=ACT.Identity, bias=bias_sb[:, 0:1], scale=1.0,
                )

        stored = {"c": 0}

        def store(c):
            w0, n = chunks[c]
            done = 20 * (w0 + n)
            c0 = stored["c"]
            c1 = c0
            while c1 < 64 and CPITCH * c1 + 800 <= done:
                c1 += 1
            stored["c"] = c1
            a = c0
            while a < c1:
                lap = (CPITCH * a) // RINGF
                pos = CPITCH * a - lap * RINGF
                if (CPITCH * a + 799) // RINGF != lap:
                    k = RINGF - pos
                    nc.sync.dma_start(out=of[a // 32, :, (a % 32) * 800:(a % 32) * 800 + k], in_=ring[:, pos:RINGF])
                    nc.sync.dma_start(out=of[a // 32, :, (a % 32) * 800 + k:(a % 32 + 1) * 800], in_=ring[:, 0:800 - k])
                    a += 1
                    continue
                b = a + 1
                while b < c1 and b // 32 == a // 32 and (CPITCH * b + 799) // RINGF == lap:
                    b += 1
                nc.sync.dma_start(
                    out=of[a // 32, :, (a % 32) * 800:(a % 32 + b - a) * 800].rearrange("o (c e) -> o c e", e=800),
                    in_=ring[:, pos:pos + CPITCH * (b - a)].rearrange("p (c e) -> p c e", e=CPITCH)[:, :, 0:800],
                )
                a = b

        diff = const.tile([P, P], I32)
        nc.gpsimd.iota(diff[:], pattern=[[1, 32], [1, 4]], base=0, channel_multiplier=-1)
        sels = []
        for jb in range(5):
            sel = const.tile([P, P], BF16, name="sel%d" % jb)
            nc.vector.tensor_scalar(
                out=sel[:], in0=diff[:], scalar1=float(-ROW0[jb]), scalar2=None, op0=ALU.is_equal,
            )
            sels.append(sel)
        xl = {"n": 16}
        for j in range(2):
            load_x(j)
        nc.scalar.activation(out=bias_sb[:], in_=zb[:, 0:1], func=ACT.Identity, bias=0.0, scale=1.0)
        w_view = weights.rearrange("(m i j) o -> j m i o", i=4, j=4)
        for dj in range(4):
            nc.scalar.dma_start(out=raw_w[dj:P:4, :, :], in_=w_view[dj])
        nc.scalar.dma_start(out=zb[0:1, :], in_=bias.rearrange("(o c) -> o c", o=1))
        for j in range(2, xl["n"]):
            load_x(j)

        st = {"pe": 0, "out": 0}

        def t_pe():
            if st["pe"] < NG:
                transposes_pe(st["pe"])
                st["pe"] += 1

        def t_take():
            if st["out"] < NG:
                j = st["out"]
                transposes_out(j)
                st["out"] += 1
                b = (j + 1) // 2
                if b not in PESET and b not in mate and j == (4 * sum(chunks[b]) - 1) // GF:
                    park(b - 1 if b in seconds else b)
                if xl["n"] < NG:
                    load_x(xl["n"])
                    xl["n"] += 1

        t_pe()
        t_pe()
        t_take()
        t_take()
        new_xr(0)
        for jb in range(5):
            spread_jb(0, jb, jb % 2)
        overlap(0, 1)
        wg = const.tile([P, P, 4], BF16, align_bytes=64)
        nc.vector.tensor_copy(out=wg[:], in_=raw_w[:].rearrange("p i o -> p o i"))
        wcodes = const.tile([P, P], U32, align_bytes=64)
        wscales = const.tile([P, P], U8, align_bytes=64)
        nc.vector.quantize_mx(
            out=wcodes[:].bitcast(FP8X4), scales=wscales[:],
            in_=wg[:].rearrange("p o i -> p (o i)"),
        )
        copy_plane(0, 2)
        t_pe()
        t_pe()
        pb = psum_m.tile([P, 1024], BF16, name="acc")
        nc.tensor.transpose(pb[:, 0:P], zb[:], ident[:])
        nc.scalar.copy(out=bias_sb[:], in_=pb[:, 0:1])
        t_take()
        t_take()
        new_xr(1)
        for jb in range(5):
            spread_jb(1, jb, 1)
        overlap(1, 1)
        t_pe()
        t_pe()
        t_take()
        t_take()

        START = (("t", "te", "te", "t", ""), ("", "t", "te", "e", ""), ("tt", "", "e", "e", "tt"))
        LATER = ("e", "e", "", "", "tt")

        for i in range(NC):
            r = i + 2 if i + 2 < NC else None
            by_pe = r is not None and r in PESET
            late2 = i + 1 in mate
            plan = START[i] if i < len(START) else LATER

            def more(g):
                for what in plan[g]:
                    if what == "t":
                        t_pe()
                    else:
                        t_take()

            def fetch_pair():
                new_xr(r)
                overlap(mate[r], 1)
                reload(r)

            copy_plane(i, 1)
            copy_plane2_rest(i)
            if i + 1 < NC and not late2:
                copy_plane(i + 1, 2)
            if by_pe:
                new_xr(r)
            elif r == 2:
                new_xr(r)
                overlap(r, 1)
                reload(r)
            quantise(i, 0)
            if i == 1:
                t_take()
                t_take()
                fetch_pair()
            passes(i, 0)
            if i > 0:
                store(i - 1)
            more(0)
            if by_pe:
                spread_jb(r, 0, SP_ENG[0])
            quantise(i, 1)
            copy_plane(i, 3)
            if i > 1 and r in mate:
                fetch_pair()
            passes(i, 1)
            more(1)
            if by_pe:
                spread_jb(r, 1, SP_ENG[1])
            quantise(i, 2)
            passes(i, 2)
            more(2)
            if by_pe:
                spread_jb(r, 2, SP_ENG[2])
            quantise(i, 3)
            if late2:
                copy_plane(i + 1, 2)
            passes(i, 3)
            more(3)
            if by_pe:
                spread_jb(r, 3, SP_ENG[3])
            passes(i, 4)
            if by_pe:
                spread_jb(r, 4, SP_ENG[4])
            if by_pe:
                overlap(r, 1)
            more(4)
        store(NC - 1)
